import numpy as np
import ml_dtypes


def mxq(x, axis, fmt="e4m3"):
    dtype, down = {"e4m3": (ml_dtypes.float8_e4m3fn, 7), "e5m2": (ml_dtypes.float8_e5m2, 14)}[fmt]
    v = np.moveaxis(np.asarray(x, np.float32).astype(ml_dtypes.bfloat16).astype(np.float64), axis, -1)
    blocks = v.reshape(v.shape[:-1] + (-1, 32))
    amax = np.abs(blocks).max(-1, keepdims=True)
    byte = np.maximum(np.where(amax > 0, np.frexp(amax)[1] - 1 + 127, 0) - down, 1)
    scale = np.exp2(byte - 127.0)
    codes = (blocks / scale).astype(np.float32).astype(dtype).astype(np.float64)
    return np.moveaxis((codes * scale).reshape(v.shape), -1, axis)


WIDE = False


def mx_kscale(k):
    if not WIDE:
        return np.ones(k)
    levels = np.array([10, -10, 5, -5, 0])
    a = np.random.permutation(np.resize(levels, k // 512 * 4)).reshape(k // 512, 4)
    idx = np.arange(k)
    return np.exp2(a[idx // 512, idx % 128 // 32])


BF16 = ml_dtypes.bfloat16


def bf(x):
    return np.asarray(x, np.float32).astype(BF16)


def f64(x):
    return np.asarray(x).astype(np.float64)


E2M1 = np.array([0.0, 0.5, 1.0, 1.5, 2.0, 3.0, 4.0, 6.0, -0.0, -0.5, -1.0, -1.5, -2.0, -3.0, -4.0, -6.0])


def pack_weight(w, fmt):
    k, n = w.shape
    w = f64(bf(w)).reshape(k // 32, 32, n)
    amax = np.abs(w).max(1)
    if fmt == "e4m3":
        byte = np.frexp(amax)[1] - 1 + 127 - 7
    else:
        mant, ex = np.frexp(amax / 6.0)
        byte = np.where(mant > 0.5, ex, ex - 1) + 127
    byte = np.clip(np.where(amax > 0, byte, 1), 1, 254)
    scaled = (w * np.exp2(127.0 - byte)[:, None, :]).reshape(k, n).astype(np.float32)
    by_word = np.ascontiguousarray(scaled.reshape(k // 512, 128, 4, n).transpose(0, 1, 3, 2))
    if fmt == "e4m3":
        words = by_word.astype(ml_dtypes.float8_e4m3fn).view(np.uint8)
    else:
        c = by_word.astype(ml_dtypes.float4_e2m1fn).view(np.uint8) & 0xF
        words = c[..., 0::2] | (c[..., 1::2] << 4)
    return np.ascontiguousarray(words), np.ascontiguousarray(byte.astype(np.uint8).reshape(k // 512, 16, n))


def unpack_weight(words, scales, fmt):
    g, p, n, _ = words.shape
    if fmt == "e4m3":
        vals = np.ascontiguousarray(words).view(ml_dtypes.float8_e4m3fn).astype(np.float64)
    else:
        nib = np.empty((g, p, n, 4), np.uint8)
        nib[..., 0::2] = words & 0xF
        nib[..., 1::2] = words >> 4
        vals = E2M1[nib]
    vals = vals * np.repeat(np.exp2(scales.astype(np.float64) - 127.0), 8, axis=1)[..., None]
    return vals.transpose(0, 1, 3, 2).reshape(g * 512, n)

def pack4(w):
    words, scales = pack_weight(w, "e2m1")
    return words.reshape(words.shape[0], 128, -1), scales


def unpack4(words, scales):
    return unpack_weight(words.reshape(words.shape[0], 128, -1, 2), scales, "e2m1")


B, I, O, G, P = 1024, 512, 512, 5, 3
GRID_RANGE = (-1.0, 1.0)
L = G + P


def make_grid():
    h = (GRID_RANGE[1] - GRID_RANGE[0]) / G
    n = G + 2 * P + 1
    return np.linspace(GRID_RANGE[0] - P * h, GRID_RANGE[1] + P * h, n)


def b_spline(x, grid, k):
    x = x[..., None]
    g = grid[None, None, :]
    basis = ((x >= g[..., :-1]) & (x < g[..., 1:])).astype(np.float64)
    for p in range(1, k + 1):
        left_denom = g[..., p:-1] - g[..., :-(p + 1)]
        right_denom = g[..., p + 1:] - g[..., 1:-p]
        left_denom = np.where(left_denom > 0, left_denom, np.ones_like(left_denom))
        right_denom = np.where(right_denom > 0, right_denom, np.ones_like(right_denom))
        left = (x - g[..., :-(p + 1)]) / left_denom * basis[..., :-1]
        right = (g[..., p + 1:] - x) / right_denom * basis[..., 1:]
        basis = left + right
    return basis


def setup_inputs():
    s = mx_kscale(I)
    s = s / s.max()
    x = bf(np.random.uniform(-1.0, 1.0, (B, I)) * s)
    base_weight = np.random.uniform(-1.0, 1.0, (O, I)) * 3.0 / np.sqrt(I) / s
    base_weight_words, base_weight_scales = pack4(np.ascontiguousarray(base_weight.T))
    spline_weight = bf(np.random.standard_normal((O, I, L)) * 1.5 / np.sqrt(I))
    return {"x": x,
            "base_weight_words": base_weight_words,
            "base_weight_scales": base_weight_scales,
            "spline_weight": spline_weight}


def reference(x, base_weight_words, base_weight_scales, spline_weight):
    x = f64(x)
    grid = make_grid()
    scale_base, scale_spline = 1.0, 1.0
    base_out = mxq(x, 1, "e4m3") @ unpack4(base_weight_words, base_weight_scales)
    basis = b_spline(x, grid, P)
    spline_out = mxq(basis.reshape(B, I * L), 1, "e4m3") @ mxq(f64(spline_weight).reshape(O, I * L), 1, "e4m3").T
    return scale_base * base_out + scale_spline * spline_out

@@ -1,0 +1,258 @@
+from contextlib import ExitStack
+import math
+
+import concourse.mybir as mybir
+from concourse.masks import make_identity
+
+F32 = mybir.dt.float32
+BF16 = mybir.dt.bfloat16
+U8 = mybir.dt.uint8
+U32 = mybir.dt.uint32
+I32 = mybir.dt.int32
+FP8X4 = mybir.dt.float8_e4m3fn_x4
+FP4X4 = mybir.dt.float4_e2m1fn_x4
+ALU = mybir.AluOpType
+ACT = mybir.ActivationFunctionType
+
+P = 128
+B, I, O, L = 1024, 512, 512, 8
+FLOPS = 2 * B * O * (I + I * L)
+
+W = 4 * P
+UNITS = B // P
+S6 = 1.0 / math.sqrt(6.0)
+
+
+def tile_kanlayer_kernel(tc, x, base_weight_words, base_weight_scales, spline_weight, out):
+    nc = tc.nc
+    with ExitStack() as ctx:
+        keep = ctx.enter_context(tc.tile_pool(name="keep", bufs=1))
+        chain = ctx.enter_context(tc.tile_pool(name="chain", bufs=3))
+        dve = ctx.enter_context(tc.tile_pool(name="dve", bufs=2))
+        grp = ctx.enter_context(tc.tile_pool(name="grp", bufs=8))
+        tps = ctx.enter_context(tc.psum_pool(name="tps", bufs=4))
+        accs = ctx.enter_context(tc.psum_pool(name="accs", bufs=4))
+        ctx.enter_context(tc.manual_schedule())
+
+        w4s = keep.tile([P, O], U8, name="w4s", align_bytes=64)
+        nc.vector.memset(w4s[:].bitcast(I32), 0)
+        ident_bf = keep.tile([P, P], BF16, name="ident_bf")
+        make_identity(nc, ident_bf[:])
+        ident_f = keep.tile([P, P], F32, name="ident_f")
+        make_identity(nc, ident_f[:])
+
+        x2 = keep.tile([P, 32, P], BF16, name="x2")
+        x2_src = x.rearrange("(n bl) (t p) -> (bl t) n p", bl=32, t=4)
+        sw2 = keep.tile([P, 16, 1024], BF16, name="sw2")
+        sw2_src = spline_weight.rearrange("(m ol) (t p) l -> (ol t) m (p l)", ol=32, t=4)
+        xb = keep.tile([P, 8, I], BF16, name="xb")
+        w4 = keep.tile([P, 2 * O], U8, name="w4", align_bytes=64)
+
+        def load_x2(a, b):
+            nc.sync.dma_start(out=x2[:, a:b, :], in_=x2_src[:, a:b, :])
+
+        def load_sw(g):
+            nc.sync.dma_start(out=sw2[:, 4 * g:4 * g + 4, :], in_=sw2_src[:, 4 * g:4 * g + 4, :])
+
+        load_x2(0, 8)
+        load_sw(0)
+        load_x2(8, 16)
+        load_sw(1)
+        load_x2(16, 32)
+        load_sw(2)
+        load_sw(3)
+        nc.sync.dma_start(out=xb[:], in_=x.rearrange("(n b) i -> b n i", b=P))
+        nc.sync.dma_start(out=w4[:].bitcast(I32), in_=base_weight_words[0].bitcast(I32))
+        for q in range(4):
+            nc.sync.dma_start(
+                out=w4s[32 * q:32 * q + 4, :].bitcast(I32),
+                in_=base_weight_scales[0, 4 * q:4 * q + 4, :].bitcast(I32),
+            )
+
+        xg = keep.tile([P, 4 * B], BF16, name="xg", align_bytes=64)
+        swc = keep.tile([P, L, O], U32, name="swc", align_bytes=64)
+        sws = keep.tile([P, L, O], U8, name="sws", align_bytes=64)
+        xc = keep.tile([P, B], U32, name="xc", align_bytes=64)
+        xs = keep.tile([P, B], U8, name="xs", align_bytes=64)
+        xbg = keep.tile([P, B, 2], F32, name="xbg", align_bytes=64)
+
+        def x_turn(k):
+            xt = tps.tile([P, 2 * W], BF16, name="xt", tag="tp")
+            for j in range(8):
+                nc.tensor.transpose(xt[:, j * P:(j + 1) * P], x2[:, 8 * k + j, :], ident_bf[:])
+            nc.scalar.copy(out=xg[:, 2 * k * W:2 * (k + 1) * W], in_=xt[:])
+
+        sw_tiles = {}
+
+        def w_turn(i):
+            h, l = divmod(i, L)
+            st = tps.tile([P, 8 * P], BF16, name="st", tag="tp")
+            for j in range(8):
+                nc.tensor.transpose(st[:, j * P:(j + 1) * P], sw2[:, 8 * h + j, l:1024:8], ident_bf[:])
+            swg = grp.tile([P, 8 * P], BF16, name="swg", align_bytes=64)
+            nc.scalar.copy(out=swg[:], in_=st[:])
+            sw_tiles[i] = swg
+
+        def w_quant(i):
+            h, l = divmod(i, L)
+            nc.vector.quantize_mx(
+                out=swc[:, l, h * 256:(h + 1) * 256].bitcast(FP8X4),
+                scales=sws[:, l, h * 256:(h + 1) * 256],
+                in_=sw_tiles[i][:],
+            )
+
+        def base_turn():
+            for n2 in range(4):
+                bt = tps.tile([P, 2, 2, P], F32, name="bt", tag="tp")
+                for dn in range(2):
+                    words = xb[:, 2 * n2 + dn, :].bitcast(F32)
+                    for u in range(2):
+                        nc.tensor.transpose(bt[:, dn, u, :], words[:, u:256:2], ident_f[:])
+                nc.scalar.copy(
+                    out=xbg[:, 2 * n2 * P:(2 * n2 + 2) * P, :].rearrange("p (dn b) u -> p dn b u", dn=2),
+                    in_=bt[:].rearrange("p dn u b -> p dn b u"),
+                )
+
+        def base_quant():
+            nc.vector.quantize_mx(
+                out=xc[:].bitcast(FP8X4),
+                scales=xs[:],
+                in_=xbg[:].rearrange("p b u -> p (b u)").bitcast(BF16),
+            )
+
+        chains = {}
+
+        def flat(t):
+            return t[:].rearrange("p c w -> p (c w)")
+
+        def act_chain(u):
+            xk = xg[:, u * W:(u + 1) * W]
+            t1 = chain.tile([P, 2, W], F32, name="t1")
+            t2 = chain.tile([P, 2, W], F32, name="t2")
+            t3 = chain.tile([P, 2, W], F32, name="t3")
+            for c in range(2):
+                nc.scalar.activation(out=t1[:, c, :], in_=xk, func=ACT.Abs, scale=2.5, bias=-0.5 - c)
+            nc.scalar.activation(out=flat(t1), in_=flat(t1), func=ACT.Abs, scale=1.0, bias=-2.0)
+            for c in range(2):
+                nc.scalar.activation(out=t2[:, 1 - c, :], in_=t1[:, c, :], func=ACT.Abs, scale=1.0, bias=-1.0)
+            nc.scalar.activation(out=flat(t3), in_=flat(t2), func=ACT.Square, scale=S6)
+            nc.scalar.activation(out=flat(t1), in_=flat(t1), func=ACT.Copy, scale=1.0, bias=-1.0)
+            chains[u] = (t1, t2, t3)
+
+        codes = {}
+
+        def dve_unit(u, split_quant=False):
+            xk = xg[:, u * W:(u + 1) * W]
+            t1, t2, t3 = chains[u]
+            tau = dve.tile([P, 4, W], BF16, name="tau")
+            for r in range(4):
+                nc.vector.tensor_scalar(out=tau[:, r, :], in0=xk, scalar1=0.4 * r - 0.6, scalar2=0.5,
+                                        op0=(ALU.is_ge if r < 2 else ALU.is_lt), op1=ALU.subtract)
+            for c in range(2):
+                nc.vector.scalar_tensor_tensor(out=t1[:, c, :], in0=t3[:, 1 - c, :], scalar=0.5, in1=t1[:, c, :],
+                                               op0=ALU.subtract, op1=ALU.mult)
+            nc.vector.scalar_tensor_tensor(out=flat(t2), in0=flat(t2), scalar=0.5, in1=flat(t3),
+                                           op0=ALU.mult, op1=ALU.mult)
+            y = dve.tile([P, 4, W], BF16, name="y")
+            nc.vector.scalar_tensor_tensor(out=y[:, 0:2, :].rearrange("p c w -> p (c w)"), in0=flat(t1), scalar=0.0,
+                                           in1=flat(t2), op0=ALU.min, op1=ALU.subtract)
+            nc.vector.scalar_tensor_tensor(out=y[:, 2:4, :].rearrange("p c w -> p (c w)"), in0=flat(t1), scalar=0.0,
+                                           in1=flat(t2), op0=ALU.max, op1=ALU.add)
+            nc.vector.tensor_tensor(out=flat(y), in0=flat(y), in1=flat(tau), op=ALU.mult)
+            planes = dve.tile([P, L, W], BF16, name="planes", align_bytes=64)
+            bc = keep.tile([P, L, P], U32, name="bc%d" % u, align_bytes=64)
+            bs = keep.tile([P, L, P], U8, name="bs%d" % u, align_bytes=64)
+            codes[u] = (bc, bs)
+            for h in range(2):
+                nc.vector.tensor_scalar(out=planes[:, 4 * h:4 * h + 4, :].rearrange("p l w -> p (l w)"), in0=flat(y),
+                                        scalar1=(4.0 if h == 0 else -4.0), scalar2=0.0, op0=ALU.mult, op1=ALU.max)
+                if split_quant:
+                    nc.vector.quantize_mx(
+                        out=bc[:, 4 * h:4 * h + 4, :].rearrange("p l w -> p (l w)").bitcast(FP8X4),
+                        scales=bs[:, 4 * h:4 * h + 4, :].rearrange("p l w -> p (l w)"),
+                        in_=planes[:, 4 * h:4 * h + 4, :].rearrange("p l w -> p (l w)"),
+                    )
+            if not split_quant:
+                nc.vector.quantize_mx(out=flat(bc).bitcast(FP8X4), scales=flat(bs), in_=flat(planes))
+
+        accd = {}
+
+        def product(u):
+            bc, bs = codes[u]
+            acc = accs.tile([P, O], F32, name="acc")
+            nc.tensor.matmul_mx(
+                out=acc[:],
+                lhsT=xc[:, u * P:(u + 1) * P].bitcast(FP8X4),
+                lhsT_scale=xs[:, u * P:(u + 1) * P],
+                rhs=w4[:].bitcast(FP4X4),
+                rhs_scale=w4s[:],
+                start=True,
+                stop=False,
+            )
+            for l in range(L):
+                nc.tensor.matmul_mx(
+                    out=acc[:],
+                    lhsT=bc[:, l, :].bitcast(FP8X4),
+                    lhsT_scale=bs[:, l, :],
+                    rhs=swc[:, l, :].bitcast(FP8X4),
+                    rhs_scale=sws[:, l, :],
+                    start=False,
+                    stop=(l == L - 1),
+                )
+            accd[u] = acc
+
+        def result(u):
+            res = dve.tile([P, O], F32, name="res", bufs=3)
+            nc.scalar.copy(out=res[:], in_=accd[u][:])
+            nc.sync.dma_start(out=out[u * P:(u + 1) * P, :], in_=res[:])
+
+        x_turn(0)
+        act_chain(0)
+        act_chain(1)
+        x_turn(1)
+        dve_unit(0)
+        for i in range(0, 4):
+            w_turn(i)
+        act_chain(2)
+        for i in range(0, 4):
+            w_quant(i)
+        dve_unit(1)
+        x_turn(2)
+        for i in range(4, 8):
+            w_turn(i)
+        act_chain(3)
+        for i in range(4, 8):
+            w_quant(i)
+        dve_unit(2)
+        x_turn(3)
+        for i in range(8, 12):
+            w_turn(i)
+        act_chain(4)
+        for i in range(8, 12):
+            w_quant(i)
+        dve_unit(3)
+        for i in range(12, 16):
+            w_turn(i)
+        base_turn()
+        act_chain(5)
+        for i in range(12, 16):
+            w_quant(i)
+        base_quant()
+        dve_unit(4)
+        for u in range(4):
+            product(u)
+        act_chain(6)
+        for u in range(4):
+            result(u)
+        dve_unit(5)
+        product(4)
+        product(5)
+        act_chain(7)
+        result(4)
+        result(5)
+        dve_unit(6)
+        product(6)
+        result(6)
+        dve_unit(7, split_quant=True)
+        product(7)
+        result(7)

@@ -80,7 +80,7 @@ def tile_kanlayer_kernel(tc, x, base_weight_words, base_weight_scales, spline_we
             xt = tps.tile([P, 2 * W], BF16, name="xt", tag="tp")
             for j in range(8):
                 nc.tensor.transpose(xt[:, j * P:(j + 1) * P], x2[:, 8 * k + j, :], ident_bf[:])
-            nc.scalar.copy(out=xg[:, 2 * k * W:2 * (k + 1) * W], in_=xt[:])
+            nc.scalar.copy(out=xg[:, 2 * k * W:2 * (k + 1) * W].bitcast(F32), in_=xt[:].bitcast(F32))
 
         sw_tiles = {}
 
@@ -90,7 +90,7 @@ def tile_kanlayer_kernel(tc, x, base_weight_words, base_weight_scales, spline_we
             for j in range(8):
                 nc.tensor.transpose(st[:, j * P:(j + 1) * P], sw2[:, 8 * h + j, l:1024:8], ident_bf[:])
             swg = grp.tile([P, 8 * P], BF16, name="swg", align_bytes=64)
-            nc.scalar.copy(out=swg[:], in_=st[:])
+            nc.scalar.copy(out=swg[:].bitcast(F32), in_=st[:].bitcast(F32))
             sw_tiles[i] = swg
 
         def w_quant(i):
@@ -125,55 +125,80 @@ def tile_kanlayer_kernel(tc, x, base_weight_words, base_weight_scales, spline_we
         def flat(t):
             return t[:].rearrange("p c w -> p (c w)")
 
-        def act_chain(u):
-            xk = xg[:, u * W:(u + 1) * W]
-            t1 = chain.tile([P, 2, W], F32, name="t1")
-            t2 = chain.tile([P, 2, W], F32, name="t2")
-            t3 = chain.tile([P, 2, W], F32, name="t3")
-            for c in range(2):
-                nc.scalar.activation(out=t1[:, c, :], in_=xk, func=ACT.Abs, scale=2.5, bias=-0.5 - c)
-            nc.scalar.activation(out=flat(t1), in_=flat(t1), func=ACT.Abs, scale=1.0, bias=-2.0)
-            for c in range(2):
-                nc.scalar.activation(out=t2[:, 1 - c, :], in_=t1[:, c, :], func=ACT.Abs, scale=1.0, bias=-1.0)
-            nc.scalar.activation(out=flat(t3), in_=flat(t2), func=ACT.Square, scale=S6)
-            nc.scalar.activation(out=flat(t1), in_=flat(t1), func=ACT.Copy, scale=1.0, bias=-1.0)
-            chains[u] = (t1, t2, t3)
+        def new_chain(u):
+            chains[u] = (
+                chain.tile([P, 2, W], F32, name="t1"),
+                chain.tile([P, 2, W], F32, name="t2"),
+                chain.tile([P, 2, W], F32, name="t3"),
+            )
 
+        def act_chain(u, c0=0, c1=W):
+            xk = xg[:, u * W + c0:u * W + c1]
+            t1, t2, t3 = chains[u]
+            for c in range(2):
+                nc.scalar.activation(out=t1[:, c, c0:c1], in_=xk, func=ACT.Abs, scale=2.5, bias=-0.5 - c)
+            for c in range(2):
+                nc.scalar.activation(out=t1[:, c, c0:c1], in_=t1[:, c, c0:c1], func=ACT.Abs, scale=1.0, bias=-2.0)
+            for c in range(2):
+                nc.scalar.activation(out=t2[:, 1 - c, c0:c1], in_=t1[:, c, c0:c1], func=ACT.Abs, scale=1.0, bias=-1.0)
+            for c in range(2):
+                nc.scalar.activation(out=t1[:, c, c0:c1], in_=t1[:, c, c0:c1], func=ACT.Copy, scale=1.0, bias=-1.0)
+            for c in range(2):
+                nc.scalar.activation(out=t3[:, 1 - c, c0:c1], in_=t2[:, 1 - c, c0:c1], func=ACT.Square, scale=S6)
+
+        ys = {}
+        taus = {}
         codes = {}
 
-        def dve_unit(u, split_quant=False):
+        def d_tau(u):
             xk = xg[:, u * W:(u + 1) * W]
-            t1, t2, t3 = chains[u]
             tau = dve.tile([P, 4, W], BF16, name="tau")
             for r in range(4):
                 nc.vector.tensor_scalar(out=tau[:, r, :], in0=xk, scalar1=0.4 * r - 0.6, scalar2=0.5,
                                         op0=(ALU.is_ge if r < 2 else ALU.is_lt), op1=ALU.subtract)
+            taus[u] = tau
+
+        def d_kc(u, c0=0, c1=W):
+            t1, t2, t3 = chains[u]
             for c in range(2):
-                nc.vector.scalar_tensor_tensor(out=t1[:, c, :], in0=t3[:, 1 - c, :], scalar=0.5, in1=t1[:, c, :],
-                                               op0=ALU.subtract, op1=ALU.mult)
-            nc.vector.scalar_tensor_tensor(out=flat(t2), in0=flat(t2), scalar=0.5, in1=flat(t3),
+                nc.vector.scalar_tensor_tensor(out=t1[:, c, c0:c1], in0=t3[:, 1 - c, c0:c1], scalar=0.5,
+                                               in1=t1[:, c, c0:c1], op0=ALU.subtract, op1=ALU.mult)
+            nc.vector.scalar_tensor_tensor(out=t2[:, :, c0:c1], in0=t2[:, :, c0:c1], scalar=0.5, in1=t3[:, :, c0:c1],
                                            op0=ALU.mult, op1=ALU.mult)
-            y = dve.tile([P, 4, W], BF16, name="y")
-            nc.vector.scalar_tensor_tensor(out=y[:, 0:2, :].rearrange("p c w -> p (c w)"), in0=flat(t1), scalar=0.0,
-                                           in1=flat(t2), op0=ALU.min, op1=ALU.subtract)
-            nc.vector.scalar_tensor_tensor(out=y[:, 2:4, :].rearrange("p c w -> p (c w)"), in0=flat(t1), scalar=0.0,
-                                           in1=flat(t2), op0=ALU.max, op1=ALU.add)
-            nc.vector.tensor_tensor(out=flat(y), in0=flat(y), in1=flat(tau), op=ALU.mult)
-            planes = dve.tile([P, L, W], BF16, name="planes", align_bytes=64)
-            bc = keep.tile([P, L, P], U32, name="bc%d" % u, align_bytes=64)
-            bs = keep.tile([P, L, P], U8, name="bs%d" % u, align_bytes=64)
-            codes[u] = (bc, bs)
-            for h in range(2):
-                nc.vector.tensor_scalar(out=planes[:, 4 * h:4 * h + 4, :].rearrange("p l w -> p (l w)"), in0=flat(y),
-                                        scalar1=(4.0 if h == 0 else -4.0), scalar2=0.0, op0=ALU.mult, op1=ALU.max)
-                if split_quant:
-                    nc.vector.quantize_mx(
-                        out=bc[:, 4 * h:4 * h + 4, :].rearrange("p l w -> p (l w)").bitcast(FP8X4),
-                        scales=bs[:, 4 * h:4 * h + 4, :].rearrange("p l w -> p (l w)"),
-                        in_=planes[:, 4 * h:4 * h + 4, :].rearrange("p l w -> p (l w)"),
-                    )
-            if not split_quant:
-                nc.vector.quantize_mx(out=flat(bc).bitcast(FP8X4), scales=flat(bs), in_=flat(planes))
+
+        def d_y(u, c0=0, c1=W):
+            t1, t2, t3 = chains[u]
+            if u not in ys:
+                ys[u] = dve.tile([P, 4, W], BF16, name="y")
+            y = ys[u]
+            nc.vector.scalar_tensor_tensor(out=y[:, 0:2, c0:c1], in0=t1[:, :, c0:c1], scalar=0.0, in1=t2[:, :, c0:c1],
+                                           op0=ALU.min, op1=ALU.subtract)
+            nc.vector.scalar_tensor_tensor(out=y[:, 2:4, c0:c1], in0=t1[:, :, c0:c1], scalar=0.0, in1=t2[:, :, c0:c1],
+                                           op0=ALU.max, op1=ALU.add)
+
+        def d_mul(u):
+            nc.vector.tensor_tensor(out=flat(ys[u]), in0=flat(ys[u]), in1=flat(taus[u]), op=ALU.mult)
+
+        planes_of = {}
+
+        def d_split(u, h):
+            if u not in planes_of:
+                planes_of[u] = dve.tile([P, L, W], BF16, name="planes", align_bytes=64)
+                codes[u] = (
+                    keep.tile([P, L, P], U32, name="bc%d" % u, align_bytes=64),
+                    keep.tile([P, L, P], U8, name="bs%d" % u, align_bytes=64),
+                )
+            nc.vector.tensor_scalar(out=planes_of[u][:, 4 * h:4 * h + 4, :].rearrange("p l w -> p (l w)"),
+                                    in0=flat(ys[u]), scalar1=(4.0 if h == 0 else -4.0), scalar2=0.0,
+                                    op0=ALU.mult, op1=ALU.max)
+
+        def d_quant(u, l0=0, l1=L):
+            bc, bs = codes[u]
+            nc.vector.quantize_mx(
+                out=bc[:, l0:l1, :].rearrange("p l w -> p (l w)").bitcast(FP8X4),
+                scales=bs[:, l0:l1, :].rearrange("p l w -> p (l w)"),
+                in_=planes_of[u][:, l0:l1, :].rearrange("p l w -> p (l w)"),
+            )
 
         accd = {}
 
@@ -206,53 +231,79 @@ def tile_kanlayer_kernel(tc, x, base_weight_words, base_weight_scales, spline_we
             nc.scalar.copy(out=res[:], in_=accd[u][:])
             nc.sync.dma_start(out=out[u * P:(u + 1) * P, :], in_=res[:])
 
+        def ahead(n):
+            if n == 0:
+                new_chain(2)
+                act_chain(2)
+                for i in range(0, 4):
+                    w_turn(i)
+            elif n == 1:
+                x_turn(2)
+                new_chain(3)
+                act_chain(3)
+                for i in range(4, 8):
+                    w_turn(i)
+            elif n == 2:
+                x_turn(3)
+                new_chain(4)
+                act_chain(4)
+                for i in range(8, 12):
+                    w_turn(i)
+            elif n == 3:
+                new_chain(5)
+                act_chain(5)
+                for i in range(12, 16):
+                    w_turn(i)
+            elif n == 4:
+                base_turn()
+                new_chain(6)
+                act_chain(6)
+            elif n == 5:
+                new_chain(7)
+                act_chain(7)
+
+        H = W // 2
         x_turn(0)
-        act_chain(0)
+        new_chain(0)
+        act_chain(0, 0, H)
+        act_chain(0, H, W)
+        new_chain(1)
         act_chain(1)
         x_turn(1)
-        dve_unit(0)
-        for i in range(0, 4):
-            w_turn(i)
-        act_chain(2)
-        for i in range(0, 4):
-            w_quant(i)
-        dve_unit(1)
-        x_turn(2)
-        for i in range(4, 8):
-            w_turn(i)
-        act_chain(3)
-        for i in range(4, 8):
-            w_quant(i)
-        dve_unit(2)
-        x_turn(3)
-        for i in range(8, 12):
-            w_turn(i)
-        act_chain(4)
-        for i in range(8, 12):
-            w_quant(i)
-        dve_unit(3)
-        for i in range(12, 16):
-            w_turn(i)
-        base_turn()
-        act_chain(5)
-        for i in range(12, 16):
-            w_quant(i)
-        base_quant()
-        dve_unit(4)
-        for u in range(4):
-            product(u)
-        act_chain(6)
-        for u in range(4):
+        done = 0
+        for n in range(UNITS + 1):
+            ahead(n)
+            if n == 0:
+                d_tau(0)
+                d_kc(0, 0, H)
+                d_y(0, 0, H)
+                d_kc(0, H, W)
+                d_y(0, H, W)
+                continue
+            if 2 <= n <= 5:
+                for i in range(4 * (n - 2), 4 * (n - 2) + 4):
+                    w_quant(i)
+            if n == 5:
+                base_quant()
+            if n < UNITS:
+                d_kc(n)
+            d_mul(n - 1)
+            if n < UNITS:
+                d_y(n)
+                d_split(n - 1, 0)
+                d_split(n - 1, 1)
+                d_tau(n)
+                d_quant(n - 1)
+            else:
+                d_split(n - 1, 0)
+                d_quant(n - 1, 0, 4)
+                d_split(n - 1, 1)
+                d_quant(n - 1, 4, 8)
+            if n >= 5:
+                while done <= n - 1:
+                    product(done)
+                    if done >= 3:
+                        result(done - 3)
+                    done += 1
+        for u in range(UNITS - 3, UNITS):
             result(u)
-        dve_unit(5)
-        product(4)
-        product(5)
-        act_chain(7)
-        result(4)
-        result(5)
-        dve_unit(6)
-        product(6)
-        result(6)
-        dve_unit(7, split_quant=True)
-        product(7)
-        result(7)

@@ -21,6 +21,7 @@ FLOPS = 2 * B * O * (I + I * L)
 W = 4 * P
 UNITS = B // P
 S6 = 1.0 / math.sqrt(6.0)
+PLANE_AT = (0, 1, 4, 5, 2, 3, 6, 7)
 
 
 def tile_kanlayer_kernel(tc, x, base_weight_words, base_weight_scales, spline_weight, out):
@@ -54,7 +55,8 @@ def tile_kanlayer_kernel(tc, x, base_weight_words, base_weight_scales, spline_we
         def load_sw(g):
             nc.sync.dma_start(out=sw2[:, 4 * g:4 * g + 4, :], in_=sw2_src[:, 4 * g:4 * g + 4, :])
 
-        load_x2(0, 8)
+        load_x2(0, 4)
+        load_x2(4, 8)
         load_sw(0)
         load_x2(8, 16)
         load_sw(1)
@@ -76,11 +78,11 @@ def tile_kanlayer_kernel(tc, x, base_weight_words, base_weight_scales, spline_we
         xs = keep.tile([P, B], U8, name="xs", align_bytes=64)
         xbg = keep.tile([P, B, 2], F32, name="xbg", align_bytes=64)
 
-        def x_turn(k):
-            xt = tps.tile([P, 2 * W], BF16, name="xt", tag="tp")
-            for j in range(8):
-                nc.tensor.transpose(xt[:, j * P:(j + 1) * P], x2[:, 8 * k + j, :], ident_bf[:])
-            nc.scalar.copy(out=xg[:, 2 * k * W:2 * (k + 1) * W].bitcast(F32), in_=xt[:].bitcast(F32))
+        def x_turn(u0, units=2):
+            xt = tps.tile([P, units * W], BF16, name="xt", tag="tp")
+            for j in range(4 * units):
+                nc.tensor.transpose(xt[:, j * P:(j + 1) * P], x2[:, 4 * u0 + j, :], ident_bf[:])
+            nc.scalar.copy(out=xg[:, u0 * W:(u0 + units) * W].bitcast(F32), in_=xt[:].bitcast(F32))
 
         sw_tiles = {}
 
@@ -150,13 +152,13 @@ def tile_kanlayer_kernel(tc, x, base_weight_words, base_weight_scales, spline_we
         taus = {}
         codes = {}
 
-        def d_tau(u):
+        def d_tau(u, r0=0, r1=4):
             xk = xg[:, u * W:(u + 1) * W]
-            tau = dve.tile([P, 4, W], BF16, name="tau")
-            for r in range(4):
-                nc.vector.tensor_scalar(out=tau[:, r, :], in0=xk, scalar1=0.4 * r - 0.6, scalar2=0.5,
+            if u not in taus:
+                taus[u] = dve.tile([P, 4, W], BF16, name="tau")
+            for r in range(r0, r1):
+                nc.vector.tensor_scalar(out=taus[u][:, r, :], in0=xk, scalar1=0.4 * r - 0.6, scalar2=0.5,
                                         op0=(ALU.is_ge if r < 2 else ALU.is_lt), op1=ALU.subtract)
-            taus[u] = tau
 
         def d_kc(u, c0=0, c1=W):
             t1, t2, t3 = chains[u]
@@ -176,21 +178,27 @@ def tile_kanlayer_kernel(tc, x, base_weight_words, base_weight_scales, spline_we
             nc.vector.scalar_tensor_tensor(out=y[:, 2:4, c0:c1], in0=t1[:, :, c0:c1], scalar=0.0, in1=t2[:, :, c0:c1],
                                            op0=ALU.max, op1=ALU.add)
 
-        def d_mul(u):
-            nc.vector.tensor_tensor(out=flat(ys[u]), in0=flat(ys[u]), in1=flat(taus[u]), op=ALU.mult)
+        def d_mul(u, r0=0, r1=4):
+            nc.vector.tensor_tensor(out=ys[u][:, r0:r1, :].rearrange("p r w -> p (r w)"),
+                                    in0=ys[u][:, r0:r1, :].rearrange("p r w -> p (r w)"),
+                                    in1=taus[u][:, r0:r1, :].rearrange("p r w -> p (r w)"), op=ALU.mult)
 
         planes_of = {}
 
-        def d_split(u, h):
+        def d_split(u, h, on_scalar=False, g0=0, g1=2):
             if u not in planes_of:
                 planes_of[u] = dve.tile([P, L, W], BF16, name="planes", align_bytes=64)
                 codes[u] = (
                     keep.tile([P, L, P], U32, name="bc%d" % u, align_bytes=64),
                     keep.tile([P, L, P], U8, name="bs%d" % u, align_bytes=64),
                 )
-            nc.vector.tensor_scalar(out=planes_of[u][:, 4 * h:4 * h + 4, :].rearrange("p l w -> p (l w)"),
-                                    in0=flat(ys[u]), scalar1=(4.0 if h == 0 else -4.0), scalar2=0.0,
-                                    op0=ALU.mult, op1=ALU.max)
+            dst = planes_of[u][:].rearrange("p (g h r) w -> p g h (r w)", g=2, h=2)[:, g0:g1, h, :]
+            src = ys[u][:].rearrange("p (g r) w -> p g (r w)", g=2)[:, g0:g1, :]
+            if on_scalar:
+                nc.scalar.activation(out=dst, in_=src, func=ACT.Relu, scale=(4.0 if h == 0 else -4.0))
+            else:
+                nc.vector.tensor_scalar(out=dst, in0=src, scalar1=(4.0 if h == 0 else -4.0), scalar2=0.0,
+                                        op0=ALU.mult, op1=ALU.max)
 
         def d_quant(u, l0=0, l1=L):
             bc, bs = codes[u]
@@ -214,15 +222,16 @@ def tile_kanlayer_kernel(tc, x, base_weight_words, base_weight_scales, spline_we
                 start=True,
                 stop=False,
             )
-            for l in range(L):
+            for pos in range(L):
+                l = PLANE_AT[pos]
                 nc.tensor.matmul_mx(
                     out=acc[:],
-                    lhsT=bc[:, l, :].bitcast(FP8X4),
-                    lhsT_scale=bs[:, l, :],
+                    lhsT=bc[:, pos, :].bitcast(FP8X4),
+                    lhsT_scale=bs[:, pos, :],
                     rhs=swc[:, l, :].bitcast(FP8X4),
                     rhs_scale=sws[:, l, :],
                     start=False,
-                    stop=(l == L - 1),
+                    stop=(pos == L - 1),
                 )
             accd[u] = acc
 
@@ -231,79 +240,64 @@ def tile_kanlayer_kernel(tc, x, base_weight_words, base_weight_scales, spline_we
             nc.scalar.copy(out=res[:], in_=accd[u][:])
             nc.sync.dma_start(out=out[u * P:(u + 1) * P, :], in_=res[:])
 
-        def ahead(n):
-            if n == 0:
-                new_chain(2)
-                act_chain(2)
-                for i in range(0, 4):
-                    w_turn(i)
-            elif n == 1:
-                x_turn(2)
-                new_chain(3)
-                act_chain(3)
-                for i in range(4, 8):
-                    w_turn(i)
-            elif n == 2:
-                x_turn(3)
-                new_chain(4)
-                act_chain(4)
-                for i in range(8, 12):
-                    w_turn(i)
-            elif n == 3:
-                new_chain(5)
-                act_chain(5)
-                for i in range(12, 16):
-                    w_turn(i)
-            elif n == 4:
+        def turn_round(n):
+            if n in (1, 2):
+                x_turn(2 * n + 2)
+            if n == 4:
                 base_turn()
-                new_chain(6)
-                act_chain(6)
-            elif n == 5:
-                new_chain(7)
-                act_chain(7)
+            if n + 2 < UNITS:
+                new_chain(n + 2)
+                act_chain(n + 2)
+            if n <= 3:
+                for i in range(4 * n, 4 * n + 4):
+                    w_turn(i)
 
         H = W // 2
-        x_turn(0)
+        x_turn(0, 1)
         new_chain(0)
         act_chain(0, 0, H)
         act_chain(0, H, W)
+        x_turn(1, 1)
         new_chain(1)
         act_chain(1)
-        x_turn(1)
+        x_turn(2)
+        turn_round(0)
+        d_tau(0)
+        d_kc(0, 0, H)
+        d_y(0, 0, H)
+        d_kc(0, H, W)
+        d_y(0, H, W)
         done = 0
-        for n in range(UNITS + 1):
-            ahead(n)
-            if n == 0:
-                d_tau(0)
-                d_kc(0, 0, H)
-                d_y(0, 0, H)
-                d_kc(0, H, W)
-                d_y(0, H, W)
-                continue
+        for n in range(1, UNITS):
+            turn_round(n)
+            d_tau(n, 0, 2)
+            d_mul(n - 1)
+            d_tau(n, 2, 4)
+            d_split(n - 1, 1, on_scalar=(n - 1 == UNITS - 2))
+            d_split(n - 1, 0)
+            d_kc(n)
+            d_quant(n - 1)
             if 2 <= n <= 5:
                 for i in range(4 * (n - 2), 4 * (n - 2) + 4):
                     w_quant(i)
             if n == 5:
                 base_quant()
-            if n < UNITS:
-                d_kc(n)
-            d_mul(n - 1)
-            if n < UNITS:
-                d_y(n)
-                d_split(n - 1, 0)
-                d_split(n - 1, 1)
-                d_tau(n)
-                d_quant(n - 1)
-            else:
-                d_split(n - 1, 0)
-                d_quant(n - 1, 0, 4)
-                d_split(n - 1, 1)
-                d_quant(n - 1, 4, 8)
+            d_y(n)
             if n >= 5:
                 while done <= n - 1:
                     product(done)
                     if done >= 3:
                         result(done - 3)
                     done += 1
-        for u in range(UNITS - 3, UNITS):
+        last = UNITS - 1
+        d_mul(last, 0, 2)
+        d_mul(last, 2, 4)
+        d_split(last, 0, g0=0, g1=1)
+        d_split(last, 1, g0=0, g1=1)
+        d_quant(last, 0, 4)
+        d_split(last, 0, g0=1, g1=2)
+        d_split(last, 1, g0=1, g1=2)
+        d_quant(last, 4, 8)
+        product(last)
+        for u in range(UNITS - 4, UNITS):
             result(u)

@@ -21,16 +21,18 @@ FLOPS = 2 * B * O * (I + I * L)
 W = 4 * P
 UNITS = B // P
 S6 = 1.0 / math.sqrt(6.0)
-PLANE_AT = (0, 1, 4, 5, 2, 3, 6, 7)
+GATE_ON_SCALAR = (3, 4, 5, 6, 7)
+GAIN = tuple(1.0 if u in GATE_ON_SCALAR else 2.0 for u in range(UNITS))
+PLANE_AT = (0, 7, 4, 3, 2, 5, 6, 1)
 
 
 def tile_kanlayer_kernel(tc, x, base_weight_words, base_weight_scales, spline_weight, out):
     nc = tc.nc
     with ExitStack() as ctx:
         keep = ctx.enter_context(tc.tile_pool(name="keep", bufs=1))
-        chain = ctx.enter_context(tc.tile_pool(name="chain", bufs=3))
-        dve = ctx.enter_context(tc.tile_pool(name="dve", bufs=2))
+        chain = ctx.enter_context(tc.tile_pool(name="chain", bufs=2))
         grp = ctx.enter_context(tc.tile_pool(name="grp", bufs=8))
+        outs = ctx.enter_context(tc.tile_pool(name="outs", bufs=3))
         tps = ctx.enter_context(tc.psum_pool(name="tps", bufs=4))
         accs = ctx.enter_context(tc.psum_pool(name="accs", bufs=4))
         ctx.enter_context(tc.manual_schedule())
@@ -58,10 +60,10 @@ def tile_kanlayer_kernel(tc, x, base_weight_words, base_weight_scales, spline_we
         load_x2(0, 4)
         load_x2(4, 8)
         load_sw(0)
-        load_x2(8, 16)
         load_sw(1)
-        load_x2(16, 32)
+        load_x2(8, 16)
         load_sw(2)
+        load_x2(16, 32)
         load_sw(3)
         nc.sync.dma_start(out=xb[:], in_=x.rearrange("(n b) i -> b n i", b=P))
         nc.sync.dma_start(out=w4[:].bitcast(I32), in_=base_weight_words[0].bitcast(I32))
@@ -78,29 +80,34 @@ def tile_kanlayer_kernel(tc, x, base_weight_words, base_weight_scales, spline_we
         xs = keep.tile([P, B], U8, name="xs", align_bytes=64)
         xbg = keep.tile([P, B, 2], F32, name="xbg", align_bytes=64)
 
-        def x_turn(u0, units=2):
+        def copy_out(out, in_, on_vector):
+            if on_vector:
+                nc.vector.tensor_copy(out=out, in_=in_)
+            else:
+                nc.scalar.copy(out=out, in_=in_)
+
+        def x_turn(u0, units=2, on_vector=False):
             xt = tps.tile([P, units * W], BF16, name="xt", tag="tp")
             for j in range(4 * units):
                 nc.tensor.transpose(xt[:, j * P:(j + 1) * P], x2[:, 4 * u0 + j, :], ident_bf[:])
-            nc.scalar.copy(out=xg[:, u0 * W:(u0 + units) * W].bitcast(F32), in_=xt[:].bitcast(F32))
+            copy_out(xg[:, u0 * W:(u0 + units) * W].bitcast(F32), xt[:].bitcast(F32), on_vector)
 
         sw_tiles = {}
 
-        def w_turn(i):
-            h, l = divmod(i, L)
-            st = tps.tile([P, 8 * P], BF16, name="st", tag="tp")
-            for j in range(8):
-                nc.tensor.transpose(st[:, j * P:(j + 1) * P], sw2[:, 8 * h + j, l:1024:8], ident_bf[:])
+        def w_turn(l, m0, m1, on_vector=False):
+            n = m1 - m0
+            st = tps.tile([P, n * P], BF16, name="st", tag="tp")
+            for j in range(n):
+                nc.tensor.transpose(st[:, j * P:(j + 1) * P], sw2[:, m0 + j, l:1024:8], ident_bf[:])
             swg = grp.tile([P, 8 * P], BF16, name="swg", align_bytes=64)
-            nc.scalar.copy(out=swg[:].bitcast(F32), in_=st[:].bitcast(F32))
-            sw_tiles[i] = swg
+            copy_out(swg[:, 0:n * P].bitcast(F32), st[:].bitcast(F32), on_vector)
+            sw_tiles[l, m0] = swg
 
-        def w_quant(i):
-            h, l = divmod(i, L)
+        def w_quant(l, m0, m1):
             nc.vector.quantize_mx(
-                out=swc[:, l, h * 256:(h + 1) * 256].bitcast(FP8X4),
-                scales=sws[:, l, h * 256:(h + 1) * 256],
-                in_=sw_tiles[i][:],
+                out=swc[:, l, 32 * m0:32 * m1].bitcast(FP8X4),
+                scales=sws[:, l, 32 * m0:32 * m1],
+                in_=sw_tiles[l, m0][:, 0:(m1 - m0) * P],
             )
 
         def base_turn():
@@ -122,96 +129,112 @@ def tile_kanlayer_kernel(tc, x, base_weight_words, base_weight_scales, spline_we
                 in_=xbg[:].rearrange("p b u -> p (b u)").bitcast(BF16),
             )
 
-        chains = {}
+        units = {}
 
-        def flat(t):
-            return t[:].rearrange("p c w -> p (c w)")
+        class_tiles = (
+            ("v", F32, 2), ("fold", F32, 2), ("dist", F32, 1), ("sq", F32, 2), ("big32", F32, 2),
+            ("big", BF16, 2), ("gate", BF16, 2), ("side", BF16, 2), ("small", BF16, 2), ("rest", BF16, 2), ("y", BF16, 4),
+        )
 
-        def new_chain(u):
-            chains[u] = (
-                chain.tile([P, 2, W], F32, name="t1"),
-                chain.tile([P, 2, W], F32, name="t2"),
-                chain.tile([P, 2, W], F32, name="t3"),
-            )
+        def new_unit(u):
+            t = {}
+            for name, dtype, rows in class_tiles:
+                t[name] = chain.tile([P, rows, W], dtype, name=name)
+            t["planes"] = chain.tile([P, L, W], BF16, name="planes", align_bytes=64)
+            t["bc"] = keep.tile([P, L, P], U32, name="bc%d" % u, align_bytes=64)
+            t["bs"] = keep.tile([P, L, P], U8, name="bs%d" % u, align_bytes=64)
+            units[u] = t
+
+        def cols(u, name, r0, r1, c0, c1):
+            return units[u][name][:, r0:r1, c0:c1]
 
         def act_chain(u, c0=0, c1=W):
             xk = xg[:, u * W + c0:u * W + c1]
-            t1, t2, t3 = chains[u]
+            t = units[u]
             for c in range(2):
-                nc.scalar.activation(out=t1[:, c, c0:c1], in_=xk, func=ACT.Abs, scale=2.5, bias=-0.5 - c)
+                nc.scalar.activation(out=t["v"][:, c, c0:c1], in_=xk, func=ACT.Abs, scale=2.5, bias=c - 0.5)
             for c in range(2):
-                nc.scalar.activation(out=t1[:, c, c0:c1], in_=t1[:, c, c0:c1], func=ACT.Abs, scale=1.0, bias=-2.0)
+                nc.scalar.activation(out=t["fold"][:, c, c0:c1], in_=t["v"][:, c, c0:c1], func=ACT.Abs, scale=1.0, bias=-1.0)
             for c in range(2):
-                nc.scalar.activation(out=t2[:, 1 - c, c0:c1], in_=t1[:, c, c0:c1], func=ACT.Abs, scale=1.0, bias=-1.0)
-            for c in range(2):
-                nc.scalar.activation(out=t1[:, c, c0:c1], in_=t1[:, c, c0:c1], func=ACT.Copy, scale=1.0, bias=-1.0)
-            for c in range(2):
-                nc.scalar.activation(out=t3[:, 1 - c, c0:c1], in_=t2[:, 1 - c, c0:c1], func=ACT.Square, scale=S6)
+                nc.scalar.activation(out=t["sq"][:, c, c0:c1], in_=t["fold"][:, c, c0:c1], func=ACT.Square, scale=S6, bias=-S6)
+            nc.scalar.activation(out=t["dist"][:, 0, c0:c1], in_=t["fold"][:, 0, c0:c1], func=ACT.Abs, scale=1.0, bias=-1.0)
 
-        ys = {}
-        taus = {}
-        codes = {}
+        def act_gate(u, c0=0, c1=W):
+            t = units[u]
+            nc.scalar.activation(out=t["gate"][:, :, c0:c1], in_=t["v"][:, :, c0:c1], func=ACT.Sign, scale=1.0, bias=-1.0)
 
-        def d_tau(u, r0=0, r1=4):
+        def act_big(u, c0=0, c1=W):
+            t = units[u]
+            for c in range(2):
+                nc.scalar.activation(out=t["big"][:, c, c0:c1], in_=t["big32"][:, c, c0:c1], func=ACT.Copy,
+                                     scale=(3.0 if c == 0 else -3.0) * GAIN[u], bias=2.0 / 3.0 * GAIN[u])
+
+        def d_big(u, c0=0, c1=W):
+            t = units[u]
+            for c in range(2):
+                nc.vector.scalar_tensor_tensor(out=t["big32"][:, c, c0:c1], in0=t["dist"][:, 0, c0:c1],
+                                               scalar=(-2.0 if c == 0 else 1.0), in1=t["sq"][:, c, c0:c1],
+                                               op0=ALU.add, op1=ALU.mult)
+
+        def d_small(u, c0=0, c1=W):
+            t = units[u]
+            nc.vector.scalar_tensor_tensor(out=t["small"][:, :, c0:c1], in0=t["fold"][:, :, c0:c1], scalar=1.0,
+                                           in1=t["sq"][:, :, c0:c1], op0=ALU.subtract, op1=ALU.mult)
+
+        def d_gate(u, c0=0, c1=W):
+            t = units[u]
+            nc.vector.tensor_scalar(out=t["gate"][:, :, c0:c1], in0=t["v"][:, :, c0:c1], scalar1=1.0, scalar2=0.5,
+                                    op0=ALU.is_ge, op1=ALU.subtract)
+
+        def d_side(u):
             xk = xg[:, u * W:(u + 1) * W]
-            if u not in taus:
-                taus[u] = dve.tile([P, 4, W], BF16, name="tau")
-            for r in range(r0, r1):
-                nc.vector.tensor_scalar(out=taus[u][:, r, :], in0=xk, scalar1=0.4 * r - 0.6, scalar2=0.5,
-                                        op0=(ALU.is_ge if r < 2 else ALU.is_lt), op1=ALU.subtract)
+            t = units[u]
+            nc.vector.tensor_scalar(out=t["side"][:, 0, :], in0=xk, scalar1=0.2, scalar2=1.0, op0=ALU.is_lt, op1=ALU.mult)
+            nc.vector.tensor_scalar(out=t["side"][:, 1, :], in0=xk, scalar1=-0.2, scalar2=1.0, op0=ALU.is_ge, op1=ALU.mult)
 
-        def d_kc(u, c0=0, c1=W):
-            t1, t2, t3 = chains[u]
-            for c in range(2):
-                nc.vector.scalar_tensor_tensor(out=t1[:, c, c0:c1], in0=t3[:, 1 - c, c0:c1], scalar=0.5,
-                                               in1=t1[:, c, c0:c1], op0=ALU.subtract, op1=ALU.mult)
-            nc.vector.scalar_tensor_tensor(out=t2[:, :, c0:c1], in0=t2[:, :, c0:c1], scalar=0.5, in1=t3[:, :, c0:c1],
-                                           op0=ALU.mult, op1=ALU.mult)
+        def d_rest(u, c0=0, c1=W):
+            t = units[u]
+            nc.vector.tensor_scalar(out=t["rest"][:, :, c0:c1], in0=t["small"][:, :, c0:c1], scalar1=-1.0, scalar2=0.0,
+                                    op0=ALU.mult, op1=ALU.max)
 
-        def d_y(u, c0=0, c1=W):
-            t1, t2, t3 = chains[u]
-            if u not in ys:
-                ys[u] = dve.tile([P, 4, W], BF16, name="y")
-            y = ys[u]
-            nc.vector.scalar_tensor_tensor(out=y[:, 0:2, c0:c1], in0=t1[:, :, c0:c1], scalar=0.0, in1=t2[:, :, c0:c1],
-                                           op0=ALU.min, op1=ALU.subtract)
-            nc.vector.scalar_tensor_tensor(out=y[:, 2:4, c0:c1], in0=t1[:, :, c0:c1], scalar=0.0, in1=t2[:, :, c0:c1],
-                                           op0=ALU.max, op1=ALU.add)
+        def d_route(u, c0=0, c1=W):
+            t = units[u]
+            nc.vector.tensor_tensor(out=t["big"][:, :, c0:c1], in0=t["big"][:, :, c0:c1], in1=t["gate"][:, :, c0:c1], op=ALU.mult)
 
-        def d_mul(u, r0=0, r1=4):
-            nc.vector.tensor_tensor(out=ys[u][:, r0:r1, :].rearrange("p r w -> p (r w)"),
-                                    in0=ys[u][:, r0:r1, :].rearrange("p r w -> p (r w)"),
-                                    in1=taus[u][:, r0:r1, :].rearrange("p r w -> p (r w)"), op=ALU.mult)
-
-        planes_of = {}
-
-        def d_split(u, h, on_scalar=False, g0=0, g1=2):
-            if u not in planes_of:
-                planes_of[u] = dve.tile([P, L, W], BF16, name="planes", align_bytes=64)
-                codes[u] = (
-                    keep.tile([P, L, P], U32, name="bc%d" % u, align_bytes=64),
-                    keep.tile([P, L, P], U8, name="bs%d" % u, align_bytes=64),
-                )
-            dst = planes_of[u][:].rearrange("p (g h r) w -> p g h (r w)", g=2, h=2)[:, g0:g1, h, :]
-            src = ys[u][:].rearrange("p (g r) w -> p g (r w)", g=2)[:, g0:g1, :]
-            if on_scalar:
-                nc.scalar.activation(out=dst, in_=src, func=ACT.Relu, scale=(4.0 if h == 0 else -4.0))
+        def d_y(u, slot, c0=0, c1=W):
+            t = units[u]
+            if slot == 0:
+                nc.vector.tensor_tensor(out=t["y"][:, 0:2, c0:c1], in0=t["small"][:, :, c0:c1], in1=t["big"][:, :, c0:c1], op=ALU.min)
             else:
-                nc.vector.tensor_scalar(out=dst, in0=src, scalar1=(4.0 if h == 0 else -4.0), scalar2=0.0,
-                                        op0=ALU.mult, op1=ALU.max)
+                nc.vector.tensor_tensor(out=t["y"][:, 2:4, c0:c1], in0=t["rest"][:, :, c0:c1], in1=t["big"][:, :, c0:c1], op=ALU.max)
+
+        def d_planes(u, which, on_scalar=False):
+            t = units[u]
+            y, planes = t["y"], t["planes"]
+            if which < 2:
+                sign = 1.0 - 2.0 * which
+                dst = planes[:, 2 * which:2 * which + 2, :]
+                if on_scalar:
+                    nc.scalar.activation(out=dst, in_=y[:, 0:2, :], func=ACT.Relu, scale=sign)
+                else:
+                    nc.vector.tensor_scalar(out=dst, in0=y[:, 0:2, :], scalar1=sign, scalar2=0.0, op0=ALU.mult, op1=ALU.max)
+            elif which == 2:
+                nc.vector.tensor_tensor(out=planes[:, 4:6, :], in0=y[:, 2:4, :], in1=t["side"][:], op=ALU.mult)
+            else:
+                nc.vector.tensor_tensor(out=planes[:, 6:8, :], in0=y[:, 2:4, :], in1=planes[:, 4:6, :], op=ALU.subtract)
 
         def d_quant(u, l0=0, l1=L):
-            bc, bs = codes[u]
+            t = units[u]
             nc.vector.quantize_mx(
-                out=bc[:, l0:l1, :].rearrange("p l w -> p (l w)").bitcast(FP8X4),
-                scales=bs[:, l0:l1, :].rearrange("p l w -> p (l w)"),
-                in_=planes_of[u][:, l0:l1, :].rearrange("p l w -> p (l w)"),
+                out=t["bc"][:, l0:l1, :].rearrange("p l w -> p (l w)").bitcast(FP8X4),
+                scales=t["bs"][:, l0:l1, :].rearrange("p l w -> p (l w)"),
+                in_=t["planes"][:, l0:l1, :].rearrange("p l w -> p (l w)"),
             )
 
         accd = {}
 
-        def product(u):
-            bc, bs = codes[u]
+        def product(u, order=range(L)):
+            bc, bs = units[u]["bc"], units[u]["bs"]
             acc = accs.tile([P, O], F32, name="acc")
             nc.tensor.matmul_mx(
                 out=acc[:],
@@ -222,7 +245,7 @@ def tile_kanlayer_kernel(tc, x, base_weight_words, base_weight_scales, spline_we
                 start=True,
                 stop=False,
             )
-            for pos in range(L):
+            for k, pos in enumerate(order):
                 l = PLANE_AT[pos]
                 nc.tensor.matmul_mx(
                     out=acc[:],
@@ -231,73 +254,96 @@ def tile_kanlayer_kernel(tc, x, base_weight_words, base_weight_scales, spline_we
                     rhs=swc[:, l, :].bitcast(FP8X4),
                     rhs_scale=sws[:, l, :],
                     start=False,
-                    stop=(pos == L - 1),
+                    stop=(k == L - 1),
                 )
             accd[u] = acc
 
-        def result(u):
-            res = dve.tile([P, O], F32, name="res", bufs=3)
-            nc.scalar.copy(out=res[:], in_=accd[u][:])
-            nc.sync.dma_start(out=out[u * P:(u + 1) * P, :], in_=res[:])
+        def result(u, parts=1):
+            n = O // parts
+            for k in range(parts):
+                res = outs.tile([P, n], F32, name="res%d" % n)
+                copy_out(res[:], accd[u][:, k * n:(k + 1) * n], on_vector=(k == 1))
+                nc.sync.dma_start(out=out[u * P:(u + 1) * P, k * n:(k + 1) * n], in_=res[:])
 
-        def turn_round(n):
-            if n in (1, 2):
-                x_turn(2 * n + 2)
-            if n == 4:
-                base_turn()
-            if n + 2 < UNITS:
-                new_chain(n + 2)
-                act_chain(n + 2)
-            if n <= 3:
-                for i in range(4 * n, 4 * n + 4):
-                    w_turn(i)
-
+        product_at = {5: (0, 1, 2), 6: (3, 4), 7: (5, 6)}
+        result_at = {6: (0, 1), 7: (2, 3, 4)}
         H = W // 2
-        x_turn(0, 1)
-        new_chain(0)
+        w_jobs = [(l, m0, m0 + 8) for m0 in (0, 8) for l in range(L)]
+
+        def stage2(u):
+            d_route(u)
+            d_y(u, 0)
+            d_y(u, 1)
+            for which in (0, 2, 1, 3):
+                d_planes(u, which)
+
+        x_turn(0, 1, on_vector=True)
+        new_unit(0)
         act_chain(0, 0, H)
         act_chain(0, H, W)
-        x_turn(1, 1)
-        new_chain(1)
+        x_turn(1, 1, on_vector=True)
+        d_side(0)
+        for c0 in (0, H):
+            d_big(0, c0, c0 + H)
+            act_big(0, c0, c0 + H)
+            d_gate(0, c0, c0 + H)
+            d_small(0, c0, c0 + H)
+        new_unit(1)
         act_chain(1)
+        d_rest(0)
         x_turn(2)
-        turn_round(0)
-        d_tau(0)
-        d_kc(0, 0, H)
-        d_y(0, 0, H)
-        d_kc(0, H, W)
-        d_y(0, H, W)
-        done = 0
+        w_done = ()
         for n in range(1, UNITS):
-            turn_round(n)
-            d_tau(n, 0, 2)
-            d_mul(n - 1)
-            d_tau(n, 2, 4)
-            d_split(n - 1, 1, on_scalar=(n - 1 == UNITS - 2))
-            d_split(n - 1, 0)
-            d_kc(n)
+            if n in (1, 2):
+                x_turn(2 * n + 2)
+            if n == 1:
+                stage2(0)
+            if n + 1 < UNITS:
+                new_unit(n + 1)
+                act_chain(n + 1)
+            if n in GATE_ON_SCALAR:
+                act_gate(n)
+            d_big(n)
+            act_big(n)
+            now = w_jobs[4 * n - 4:4 * n]
+            for job in now:
+                w_turn(*job)
+            if n == 3:
+                base_turn()
+            if n > 1:
+                d_route(n - 1)
+            d_small(n)
+            if n > 1:
+                d_y(n - 1, 0)
+                d_y(n - 1, 1)
+            if n not in GATE_ON_SCALAR:
+                d_gate(n)
+            if n > 1:
+                for which in (0, 2, 1, 3):
+                    d_planes(n - 1, which)
+            d_side(n)
+            d_rest(n)
             d_quant(n - 1)
-            if 2 <= n <= 5:
-                for i in range(4 * (n - 2), 4 * (n - 2) + 4):
-                    w_quant(i)
-            if n == 5:
+            for job in w_done:
+                w_quant(*job)
+            w_done = now
+            if n == 4:
                 base_quant()
-            d_y(n)
-            if n >= 5:
-                while done <= n - 1:
-                    product(done)
-                    if done >= 3:
-                        result(done - 3)
-                    done += 1
+            for u in product_at.get(n, ()):
+                product(u)
+            for u in result_at.get(n, ()):
+                result(u)
         last = UNITS - 1
-        d_mul(last, 0, 2)
-        d_mul(last, 2, 4)
-        d_split(last, 0, g0=0, g1=1)
-        d_split(last, 1, g0=0, g1=1)
-        d_quant(last, 0, 4)
-        d_split(last, 0, g0=1, g1=2)
-        d_split(last, 1, g0=1, g1=2)
+        d_route(last)
+        d_y(last, 1)
+        d_y(last, 0)
+        d_planes(last, 2)
+        d_planes(last, 0, on_scalar=True)
+        d_planes(last, 1)
+        d_planes(last, 3)
         d_quant(last, 4, 8)
-        product(last)
-        for u in range(UNITS - 4, UNITS):
+        d_quant(last, 0, 4)
+        product(last, (4, 5, 6, 7, 0, 1, 2, 3))
+        for u in range(5, UNITS - 1):
             result(u)
+        result(UNITS - 1, 2)

@@ -23,6 +23,7 @@ UNITS = B // P
 S6 = 1.0 / math.sqrt(6.0)
 GATE_ON_SCALAR = (3, 4, 5, 6, 7)
 GAIN = tuple(1.0 if u in GATE_ON_SCALAR else 2.0 for u in range(UNITS))
+FIRST_REUSE = 5
 PLANE_AT = (0, 7, 4, 3, 2, 5, 6, 1)
 
 
@@ -31,10 +32,12 @@ def tile_kanlayer_kernel(tc, x, base_weight_words, base_weight_scales, spline_we
     with ExitStack() as ctx:
         keep = ctx.enter_context(tc.tile_pool(name="keep", bufs=1))
         chain = ctx.enter_context(tc.tile_pool(name="chain", bufs=2))
-        grp = ctx.enter_context(tc.tile_pool(name="grp", bufs=8))
-        outs = ctx.enter_context(tc.tile_pool(name="outs", bufs=3))
-        tps = ctx.enter_context(tc.psum_pool(name="tps", bufs=4))
-        accs = ctx.enter_context(tc.psum_pool(name="accs", bufs=4))
+        once = ctx.enter_context(tc.tile_pool(name="once", bufs=1))
+        loads = ctx.enter_context(tc.tile_pool(name="loads", bufs=4))
+        grp = ctx.enter_context(tc.tile_pool(name="grp", bufs=10))
+        outs = ctx.enter_context(tc.tile_pool(name="outs", bufs=4))
+        tps = ctx.enter_context(tc.psum_pool(name="tps", bufs=5))
+        accs = ctx.enter_context(tc.psum_pool(name="accs", bufs=3))
         ctx.enter_context(tc.manual_schedule())
 
         w4s = keep.tile([P, O], U8, name="w4s", align_bytes=64)
@@ -46,7 +49,7 @@ def tile_kanlayer_kernel(tc, x, base_weight_words, base_weight_scales, spline_we
 
         x2 = keep.tile([P, 32, P], BF16, name="x2")
         x2_src = x.rearrange("(n bl) (t p) -> (bl t) n p", bl=32, t=4)
-        sw2 = keep.tile([P, 16, 1024], BF16, name="sw2")
+        sw2 = []
         sw2_src = spline_weight.rearrange("(m ol) (t p) l -> (ol t) m (p l)", ol=32, t=4)
         xb = keep.tile([P, 8, I], BF16, name="xb")
         w4 = keep.tile([P, 2 * O], U8, name="w4", align_bytes=64)
@@ -55,15 +58,15 @@ def tile_kanlayer_kernel(tc, x, base_weight_words, base_weight_scales, spline_we
             nc.sync.dma_start(out=x2[:, a:b, :], in_=x2_src[:, a:b, :])
 
         def load_sw(g):
-            nc.sync.dma_start(out=sw2[:, 4 * g:4 * g + 4, :], in_=sw2_src[:, 4 * g:4 * g + 4, :])
+            quarter = loads.tile([P, 4, 1024], BF16, name="quarter", align_bytes=64)
+            nc.sync.dma_start(out=quarter[:], in_=sw2_src[:, 4 * g:4 * g + 4, :])
+            sw2.append(quarter)
 
         load_x2(0, 4)
-        load_x2(4, 8)
+        load_x2(4, 32)
         load_sw(0)
         load_sw(1)
-        load_x2(8, 16)
         load_sw(2)
-        load_x2(16, 32)
         load_sw(3)
         nc.sync.dma_start(out=xb[:], in_=x.rearrange("(n b) i -> b n i", b=P))
         nc.sync.dma_start(out=w4[:].bitcast(I32), in_=base_weight_words[0].bitcast(I32))
@@ -94,33 +97,33 @@ def tile_kanlayer_kernel(tc, x, base_weight_words, base_weight_scales, spline_we
 
         sw_tiles = {}
 
-        def w_turn(l, m0, m1, on_vector=False):
-            n = m1 - m0
-            st = tps.tile([P, n * P], BF16, name="st", tag="tp")
-            for j in range(n):
-                nc.tensor.transpose(st[:, j * P:(j + 1) * P], sw2[:, m0 + j, l:1024:8], ident_bf[:])
+        def w_turn(k):
+            half, l = divmod(k, L)
+            st = tps.tile([P, 8 * P], BF16, name="st", tag="tp")
+            for j in range(8):
+                nc.tensor.transpose(st[:, j * P:(j + 1) * P], sw2[2 * half + j // 4][:, j % 4, l:1024:8], ident_bf[:])
             swg = grp.tile([P, 8 * P], BF16, name="swg", align_bytes=64)
-            copy_out(swg[:, 0:n * P].bitcast(F32), st[:].bitcast(F32), on_vector)
-            sw_tiles[l, m0] = swg
+            nc.scalar.copy(out=swg[:].bitcast(F32), in_=st[:].bitcast(F32))
+            sw_tiles[k] = swg
 
-        def w_quant(l, m0, m1):
+        def w_quant(k):
+            half, l = divmod(k, L)
             nc.vector.quantize_mx(
-                out=swc[:, l, 32 * m0:32 * m1].bitcast(FP8X4),
-                scales=sws[:, l, 32 * m0:32 * m1],
-                in_=sw_tiles[l, m0][:, 0:(m1 - m0) * P],
+                out=swc[:, l, 256 * half:256 * half + 256].bitcast(FP8X4),
+                scales=sws[:, l, 256 * half:256 * half + 256],
+                in_=sw_tiles[k][:],
             )
 
-        def base_turn():
-            for n2 in range(4):
-                bt = tps.tile([P, 2, 2, P], F32, name="bt", tag="tp")
-                for dn in range(2):
-                    words = xb[:, 2 * n2 + dn, :].bitcast(F32)
-                    for u in range(2):
-                        nc.tensor.transpose(bt[:, dn, u, :], words[:, u:256:2], ident_f[:])
-                nc.scalar.copy(
-                    out=xbg[:, 2 * n2 * P:(2 * n2 + 2) * P, :].rearrange("p (dn b) u -> p dn b u", dn=2),
-                    in_=bt[:].rearrange("p dn u b -> p dn b u"),
-                )
+        def base_turn(n2):
+            bt = tps.tile([P, 2, 2, P], F32, name="bt", tag="tp")
+            for dn in range(2):
+                words = xb[:, 2 * n2 + dn, :].bitcast(F32)
+                for u in range(2):
+                    nc.tensor.transpose(bt[:, dn, u, :], words[:, u:256:2], ident_f[:])
+            nc.scalar.copy(
+                out=xbg[:, 2 * n2 * P:(2 * n2 + 2) * P, :].rearrange("p (dn b) u -> p dn b u", dn=2),
+                in_=bt[:].rearrange("p dn u b -> p dn b u"),
+            )
 
         def base_quant():
             nc.vector.quantize_mx(
@@ -131,43 +134,57 @@ def tile_kanlayer_kernel(tc, x, base_weight_words, base_weight_scales, spline_we
 
         units = {}
 
-        class_tiles = (
-            ("v", F32, 2), ("fold", F32, 2), ("dist", F32, 1), ("sq", F32, 2), ("big32", F32, 2),
-            ("big", BF16, 2), ("gate", BF16, 2), ("side", BF16, 2), ("small", BF16, 2), ("rest", BF16, 2), ("y", BF16, 4),
-        )
-
         def new_unit(u):
             t = {}
-            for name, dtype, rows in class_tiles:
-                t[name] = chain.tile([P, rows, W], dtype, name=name)
-            t["planes"] = chain.tile([P, L, W], BF16, name="planes", align_bytes=64)
-            t["bc"] = keep.tile([P, L, P], U32, name="bc%d" % u, align_bytes=64)
-            t["bs"] = keep.tile([P, L, P], U8, name="bs%d" % u, align_bytes=64)
+            for name, pool, rows, dtype in (
+                ("v", chain, 2, F32), ("fold", chain, 2, F32), ("dist", chain, 1, F32), ("sq", chain, 2, F32),
+                ("big32", chain, 2, F32), ("big", chain, 2, BF16), ("gate", chain, 2, BF16), ("small", chain, 2, BF16),
+                ("rest", once, 2, BF16), ("side", once, 2, BF16), ("y", once, 4, BF16), ("planes", once, L, BF16),
+            ):
+                t[name] = pool.tile([P, rows, W], dtype, name=name, align_bytes=64)
+            if u < FIRST_REUSE:
+                bc = keep.tile([P, L, P], U32, name="bc%d" % u, align_bytes=64)
+            else:
+                bc = loads.tile([P, L, P], U32, name="bc", tag="quarter", align_bytes=64)
+            bs = keep.tile([P, L, P], U8, name="bs%d" % u, align_bytes=64)
+            t["bc"], t["bs"] = bc, bs
             units[u] = t
 
-        def cols(u, name, r0, r1, c0, c1):
-            return units[u][name][:, r0:r1, c0:c1]
-
-        def act_chain(u, c0=0, c1=W):
+        def chain_steps(u, c0=0, c1=W):
             xk = xg[:, u * W + c0:u * W + c1]
             t = units[u]
-            for c in range(2):
-                nc.scalar.activation(out=t["v"][:, c, c0:c1], in_=xk, func=ACT.Abs, scale=2.5, bias=c - 0.5)
-            for c in range(2):
-                nc.scalar.activation(out=t["fold"][:, c, c0:c1], in_=t["v"][:, c, c0:c1], func=ACT.Abs, scale=1.0, bias=-1.0)
-            for c in range(2):
-                nc.scalar.activation(out=t["sq"][:, c, c0:c1], in_=t["fold"][:, c, c0:c1], func=ACT.Square, scale=S6, bias=-S6)
-            nc.scalar.activation(out=t["dist"][:, 0, c0:c1], in_=t["fold"][:, 0, c0:c1], func=ACT.Abs, scale=1.0, bias=-1.0)
 
-        def act_gate(u, c0=0, c1=W):
-            t = units[u]
-            nc.scalar.activation(out=t["gate"][:, :, c0:c1], in_=t["v"][:, :, c0:c1], func=ACT.Sign, scale=1.0, bias=-1.0)
+            def step(name, row, in_, func, scale, bias):
+                out_ = t[name][:, row, c0:c1]
+                return lambda: nc.scalar.activation(out=out_, in_=in_, func=func, scale=scale, bias=bias)
 
-        def act_big(u, c0=0, c1=W):
+            v, fold = t["v"], t["fold"]
+            steps = [step("v", c, xk, ACT.Abs, 2.5, c - 0.5) for c in range(2)]
+            steps += [step("fold", c, v[:, c, c0:c1], ACT.Abs, 1.0, -1.0) for c in range(2)]
+            steps += [step("sq", c, fold[:, c, c0:c1], ACT.Square, S6, -S6) for c in range(2)]
+            steps += [step("dist", 0, fold[:, 0, c0:c1], ACT.Abs, 1.0, -1.0)]
+            if u in GATE_ON_SCALAR:
+                steps += [step("gate", c, v[:, c, c0:c1], ACT.Sign, 1.0, -1.0) for c in range(2)]
+            return steps
+
+        def big_steps(u, c0=0, c1=W):
             t = units[u]
-            for c in range(2):
-                nc.scalar.activation(out=t["big"][:, c, c0:c1], in_=t["big32"][:, c, c0:c1], func=ACT.Copy,
-                                     scale=(3.0 if c == 0 else -3.0) * GAIN[u], bias=2.0 / 3.0 * GAIN[u])
+
+            def step(c):
+                return lambda: nc.scalar.activation(out=t["big"][:, c, c0:c1], in_=t["big32"][:, c, c0:c1], func=ACT.Copy,
+                                                    scale=(3.0 if c == 0 else -3.0) * GAIN[u], bias=2.0 / 3.0 * GAIN[u])
+
+            return [step(0), step(1)]
+
+        def run(steps, fills=(), every=2):
+            fills = list(fills)
+            for k, step in enumerate(steps):
+                step()
+                if k % every == every - 1 and fills:
+                    fills[0]()
+                    fills = fills[1:]
+            for fill in fills:
+                fill()
 
         def d_big(u, c0=0, c1=W):
             t = units[u]
@@ -188,40 +205,39 @@ def tile_kanlayer_kernel(tc, x, base_weight_words, base_weight_scales, spline_we
 
         def d_side(u):
             xk = xg[:, u * W:(u + 1) * W]
-            t = units[u]
-            nc.vector.tensor_scalar(out=t["side"][:, 0, :], in0=xk, scalar1=0.2, scalar2=1.0, op0=ALU.is_lt, op1=ALU.mult)
-            nc.vector.tensor_scalar(out=t["side"][:, 1, :], in0=xk, scalar1=-0.2, scalar2=1.0, op0=ALU.is_ge, op1=ALU.mult)
+            side = units[u]["side"]
+            nc.vector.tensor_scalar(out=side[:, 0, :], in0=xk, scalar1=0.2, scalar2=1.0, op0=ALU.is_lt, op1=ALU.mult)
+            nc.vector.tensor_scalar(out=side[:, 1, :], in0=xk, scalar1=-0.2, scalar2=1.0, op0=ALU.is_ge, op1=ALU.mult)
 
-        def d_rest(u, c0=0, c1=W):
+        def d_rest(u):
             t = units[u]
-            nc.vector.tensor_scalar(out=t["rest"][:, :, c0:c1], in0=t["small"][:, :, c0:c1], scalar1=-1.0, scalar2=0.0,
-                                    op0=ALU.mult, op1=ALU.max)
+            nc.vector.tensor_scalar(out=t["rest"][:], in0=t["small"][:], scalar1=-1.0, scalar2=0.0, op0=ALU.mult, op1=ALU.max)
 
-        def d_route(u, c0=0, c1=W):
+        def d_route(u):
             t = units[u]
-            nc.vector.tensor_tensor(out=t["big"][:, :, c0:c1], in0=t["big"][:, :, c0:c1], in1=t["gate"][:, :, c0:c1], op=ALU.mult)
+            nc.vector.tensor_tensor(out=t["big"][:], in0=t["big"][:], in1=t["gate"][:], op=ALU.mult)
 
-        def d_y(u, slot, c0=0, c1=W):
+        def d_y(u, slot):
             t = units[u]
             if slot == 0:
-                nc.vector.tensor_tensor(out=t["y"][:, 0:2, c0:c1], in0=t["small"][:, :, c0:c1], in1=t["big"][:, :, c0:c1], op=ALU.min)
+                nc.vector.tensor_tensor(out=t["y"][:, 0:2, :], in0=t["small"][:], in1=t["big"][:], op=ALU.min)
             else:
-                nc.vector.tensor_tensor(out=t["y"][:, 2:4, c0:c1], in0=t["rest"][:, :, c0:c1], in1=t["big"][:, :, c0:c1], op=ALU.max)
+                nc.vector.tensor_tensor(out=t["y"][:, 2:4, :], in0=t["rest"][:], in1=t["big"][:], op=ALU.max)
 
         def d_planes(u, which, on_scalar=False):
             t = units[u]
             y, planes = t["y"], t["planes"]
+            dst = planes[:, 2 * which:2 * which + 2, :]
             if which < 2:
                 sign = 1.0 - 2.0 * which
-                dst = planes[:, 2 * which:2 * which + 2, :]
                 if on_scalar:
                     nc.scalar.activation(out=dst, in_=y[:, 0:2, :], func=ACT.Relu, scale=sign)
                 else:
                     nc.vector.tensor_scalar(out=dst, in0=y[:, 0:2, :], scalar1=sign, scalar2=0.0, op0=ALU.mult, op1=ALU.max)
             elif which == 2:
-                nc.vector.tensor_tensor(out=planes[:, 4:6, :], in0=y[:, 2:4, :], in1=t["side"][:], op=ALU.mult)
+                nc.vector.tensor_tensor(out=dst, in0=y[:, 2:4, :], in1=t["side"][:], op=ALU.mult)
             else:
-                nc.vector.tensor_tensor(out=planes[:, 6:8, :], in0=y[:, 2:4, :], in1=planes[:, 4:6, :], op=ALU.subtract)
+                nc.vector.tensor_tensor(out=dst, in0=y[:, 2:4, :], in1=planes[:, 4:6, :], op=ALU.subtract)
 
         def d_quant(u, l0=0, l1=L):
             t = units[u]
@@ -268,48 +284,40 @@ def tile_kanlayer_kernel(tc, x, base_weight_words, base_weight_scales, spline_we
         product_at = {5: (0, 1, 2), 6: (3, 4), 7: (5, 6)}
         result_at = {6: (0, 1), 7: (2, 3, 4)}
         H = W // 2
-        w_jobs = [(l, m0, m0 + 8) for m0 in (0, 8) for l in range(L)]
-
-        def stage2(u):
-            d_route(u)
-            d_y(u, 0)
-            d_y(u, 1)
-            for which in (0, 2, 1, 3):
-                d_planes(u, which)
-
         x_turn(0, 1, on_vector=True)
         new_unit(0)
-        act_chain(0, 0, H)
-        act_chain(0, H, W)
+        for c0 in (0, H):
+            run(chain_steps(0, c0, c0 + H))
         x_turn(1, 1, on_vector=True)
         d_side(0)
+        x_turn(2, 2, on_vector=True)
+        x_turn(4, 2, on_vector=True)
+        x_turn(6, 2, on_vector=True)
         for c0 in (0, H):
             d_big(0, c0, c0 + H)
-            act_big(0, c0, c0 + H)
+            run(big_steps(0, c0, c0 + H))
             d_gate(0, c0, c0 + H)
             d_small(0, c0, c0 + H)
         new_unit(1)
-        act_chain(1)
+        fills_at = ((0, 1,), (2, 3, 4,), (5, 6, 7,), (8, 9, 10, 11,), (12, 13, 14, 15,), (), (), ())
+        run(chain_steps(1), [lambda k=k: w_turn(k) for k in fills_at[0]], 20)
         d_rest(0)
-        x_turn(2)
-        w_done = ()
+        d_route(0)
+        d_y(0, 0)
+        d_y(0, 1)
+        for which in (0, 2, 1, 3):
+            d_planes(0, which)
         for n in range(1, UNITS):
-            if n in (1, 2):
-                x_turn(2 * n + 2)
-            if n == 1:
-                stage2(0)
+            d_big(n)
+            steps = []
             if n + 1 < UNITS:
                 new_unit(n + 1)
-                act_chain(n + 1)
-            if n in GATE_ON_SCALAR:
-                act_gate(n)
-            d_big(n)
-            act_big(n)
-            now = w_jobs[4 * n - 4:4 * n]
-            for job in now:
-                w_turn(*job)
-            if n == 3:
-                base_turn()
+                steps = chain_steps(n + 1)
+            steps += big_steps(n)
+            fills = [lambda k=k: w_turn(k) for k in fills_at[n]]
+            if n == 4:
+                fills += [lambda k=k: base_turn(k) for k in range(4)]
+            run(steps, fills, 20)
             if n > 1:
                 d_route(n - 1)
             d_small(n)
@@ -324,26 +332,26 @@ def tile_kanlayer_kernel(tc, x, base_weight_words, base_weight_scales, spline_we
             d_side(n)
             d_rest(n)
             d_quant(n - 1)
-            for job in w_done:
-                w_quant(*job)
-            w_done = now
-            if n == 4:
+            for k in fills_at[n - 1]:
+                w_quant(k)
+            if n == 4 + 1:
                 base_quant()
-            for u in product_at.get(n, ()):
+            for u in {5: (0, 1, 2), 6: (3, 4), 7: (5, 6)}.get(n, ()):
                 product(u)
-            for u in result_at.get(n, ()):
+            for u in {6: (0, 1), 7: (2, 3, 4)}.get(n, ()):
                 result(u)
         last = UNITS - 1
         d_route(last)
-        d_y(last, 1)
         d_y(last, 0)
-        d_planes(last, 2)
+        d_y(last, 1)
         d_planes(last, 0, on_scalar=True)
+        d_planes(last, 2)
         d_planes(last, 1)
         d_planes(last, 3)
         d_quant(last, 4, 8)
-        d_quant(last, 0, 4)
-        product(last, (4, 5, 6, 7, 0, 1, 2, 3))
+        d_quant(last, 2, 4)
+        d_quant(last, 0, 2)
+        product(last, (4, 5, 6, 7, 2, 3, 0, 1))
         for u in range(5, UNITS - 1):
             result(u)
         result(UNITS - 1, 2)

@@ -63,9 +63,11 @@ def tile_kanlayer_kernel(tc, x, base_weight_words, base_weight_scales, spline_we
             sw2.append(quarter)
 
         load_x2(0, 4)
-        load_x2(4, 32)
+        load_x2(4, 8)
         load_sw(0)
         load_sw(1)
+        load_x2(8, 16)
+        load_x2(16, 32)
         load_sw(2)
         load_sw(3)
         nc.sync.dma_start(out=xb[:], in_=x.rearrange("(n b) i -> b n i", b=P))
@@ -290,9 +292,6 @@ def tile_kanlayer_kernel(tc, x, base_weight_words, base_weight_scales, spline_we
             run(chain_steps(0, c0, c0 + H))
         x_turn(1, 1, on_vector=True)
         d_side(0)
-        x_turn(2, 2, on_vector=True)
-        x_turn(4, 2, on_vector=True)
-        x_turn(6, 2, on_vector=True)
         for c0 in (0, H):
             d_big(0, c0, c0 + H)
             run(big_steps(0, c0, c0 + H))
@@ -302,12 +301,15 @@ def tile_kanlayer_kernel(tc, x, base_weight_words, base_weight_scales, spline_we
         fills_at = ((0, 1,), (2, 3, 4,), (5, 6, 7,), (8, 9, 10, 11,), (12, 13, 14, 15,), (), (), ())
         run(chain_steps(1), [lambda k=k: w_turn(k) for k in fills_at[0]], 20)
         d_rest(0)
+        x_turn(2)
         d_route(0)
         d_y(0, 0)
         d_y(0, 1)
         for which in (0, 2, 1, 3):
             d_planes(0, which)
         for n in range(1, UNITS):
+            if n in (1, 2):
+                x_turn(2 * n + 2)
             d_big(n)
             steps = []
             if n + 1 < UNITS:
@@ -315,7 +317,7 @@ def tile_kanlayer_kernel(tc, x, base_weight_words, base_weight_scales, spline_we
                 steps = chain_steps(n + 1)
             steps += big_steps(n)
             fills = [lambda k=k: w_turn(k) for k in fills_at[n]]
-            if n == 4:
+            if n == 3:
                 fills += [lambda k=k: base_turn(k) for k in range(4)]
             run(steps, fills, 20)
             if n > 1:
@@ -326,32 +328,33 @@ def tile_kanlayer_kernel(tc, x, base_weight_words, base_weight_scales, spline_we
                 d_y(n - 1, 1)
             if n not in GATE_ON_SCALAR:
                 d_gate(n)
+            for k in fills_at[n - 1]:
+                w_quant(k)
+            if n == 3 + 1:
+                base_quant()
+            for u in {5: (0, 1, 2, 3), 6: (4,), 7: (5,)}.get(n, ()):
+                product(u)
             if n > 1:
                 for which in (0, 2, 1, 3):
                     d_planes(n - 1, which)
             d_side(n)
             d_rest(n)
             d_quant(n - 1)
-            for k in fills_at[n - 1]:
-                w_quant(k)
-            if n == 4 + 1:
-                base_quant()
-            for u in {5: (0, 1, 2), 6: (3, 4), 7: (5, 6)}.get(n, ()):
-                product(u)
-            for u in {6: (0, 1), 7: (2, 3, 4)}.get(n, ()):
+            for u in {6: (0, 1), 7: (2, 3)}.get(n, ()):
                 result(u)
         last = UNITS - 1
         d_route(last)
         d_y(last, 0)
         d_y(last, 1)
-        d_planes(last, 0, on_scalar=True)
-        d_planes(last, 2)
+        d_planes(last, 0, on_scalar=False)
         d_planes(last, 1)
+        d_planes(last, 2)
+        d_quant(last, 0, 4)
         d_planes(last, 3)
-        d_quant(last, 4, 8)
-        d_quant(last, 2, 4)
-        d_quant(last, 0, 2)
-        product(last, (4, 5, 6, 7, 2, 3, 0, 1))
-        for u in range(5, UNITS - 1):
+        d_quant(last, 4, 6)
+        d_quant(last, 6, 8)
+        product(last - 1)
+        product(last)
+        for u in range(4, UNITS - 1):
             result(u)
         result(UNITS - 1, 2)

@@ -62,11 +62,12 @@ def tile_kanlayer_kernel(tc, x, base_weight_words, base_weight_scales, spline_we
             nc.sync.dma_start(out=quarter[:], in_=sw2_src[:, 4 * g:4 * g + 4, :])
             sw2.append(quarter)
 
-        load_x2(0, 4)
+        load_x2(0, 2)
+        load_x2(2, 4)
         load_x2(4, 8)
+        load_x2(8, 16)
         load_sw(0)
         load_sw(1)
-        load_x2(8, 16)
         load_x2(16, 32)
         load_sw(2)
         load_sw(3)
@@ -135,13 +136,14 @@ def tile_kanlayer_kernel(tc, x, base_weight_words, base_weight_scales, spline_we
             )
 
         units = {}
+        sides = {}
 
         def new_unit(u):
             t = {}
             for name, pool, rows, dtype in (
                 ("v", chain, 2, F32), ("fold", chain, 2, F32), ("dist", chain, 1, F32), ("sq", chain, 2, F32),
                 ("big32", chain, 2, F32), ("big", chain, 2, BF16), ("gate", chain, 2, BF16), ("small", chain, 2, BF16),
-                ("rest", once, 2, BF16), ("side", once, 2, BF16), ("y", once, 4, BF16), ("planes", once, L, BF16),
+                ("rest", once, 2, BF16), ("y", once, 4, BF16), ("planes", once, L, BF16),
             ):
                 t[name] = pool.tile([P, rows, W], dtype, name=name, align_bytes=64)
             if u < FIRST_REUSE:
@@ -152,8 +154,8 @@ def tile_kanlayer_kernel(tc, x, base_weight_words, base_weight_scales, spline_we
             t["bc"], t["bs"] = bc, bs
             units[u] = t
 
-        def chain_steps(u, c0=0, c1=W):
-            xk = xg[:, u * W + c0:u * W + c1]
+        def chain_steps(u, c0=0, c1=W, x_from=None):
+            xk = xg[:, u * W + c0:u * W + c1] if x_from is None else x_from
             t = units[u]
 
             def step(name, row, in_, func, scale, bias):
@@ -205,15 +207,21 @@ def tile_kanlayer_kernel(tc, x, base_weight_words, base_weight_scales, spline_we
             nc.vector.tensor_scalar(out=t["gate"][:, :, c0:c1], in0=t["v"][:, :, c0:c1], scalar1=1.0, scalar2=0.5,
                                     op0=ALU.is_ge, op1=ALU.subtract)
 
-        def d_side(u):
-            xk = xg[:, u * W:(u + 1) * W]
-            side = units[u]["side"]
-            nc.vector.tensor_scalar(out=side[:, 0, :], in0=xk, scalar1=0.2, scalar2=1.0, op0=ALU.is_lt, op1=ALU.mult)
-            nc.vector.tensor_scalar(out=side[:, 1, :], in0=xk, scalar1=-0.2, scalar2=1.0, op0=ALU.is_ge, op1=ALU.mult)
+        def d_side(us):
+            k = len(us)
+            xk = xg[:, us[0] * W:(us[0] + k) * W].rearrange("p (k w) -> p k w", w=W)
+            side = once.tile([P, k, 2, W], BF16, name="side")
+            nc.vector.tensor_scalar(out=side[:, :, 0, :], in0=xk, scalar1=0.2, scalar2=1.0, op0=ALU.is_lt, op1=ALU.mult)
+            nc.vector.tensor_scalar(out=side[:, :, 1, :], in0=xk, scalar1=-0.2, scalar2=1.0, op0=ALU.is_ge, op1=ALU.mult)
+            for j, u in enumerate(us):
+                sides[u] = side[:, j]
 
-        def d_rest(u):
+        def d_rest(u, on_scalar=False):
             t = units[u]
-            nc.vector.tensor_scalar(out=t["rest"][:], in0=t["small"][:], scalar1=-1.0, scalar2=0.0, op0=ALU.mult, op1=ALU.max)
+            if on_scalar:
+                nc.scalar.activation(out=t["rest"][:], in_=t["small"][:], func=ACT.Relu, scale=-1.0)
+            else:
+                nc.vector.tensor_scalar(out=t["rest"][:], in0=t["small"][:], scalar1=-1.0, scalar2=0.0, op0=ALU.mult, op1=ALU.max)
 
         def d_route(u):
             t = units[u]
@@ -237,7 +245,7 @@ def tile_kanlayer_kernel(tc, x, base_weight_words, base_weight_scales, spline_we
                 else:
                     nc.vector.tensor_scalar(out=dst, in0=y[:, 0:2, :], scalar1=sign, scalar2=0.0, op0=ALU.mult, op1=ALU.max)
             elif which == 2:
-                nc.vector.tensor_tensor(out=dst, in0=y[:, 2:4, :], in1=t["side"][:], op=ALU.mult)
+                nc.vector.tensor_tensor(out=dst, in0=y[:, 2:4, :], in1=sides[u], op=ALU.mult)
             else:
                 nc.vector.tensor_tensor(out=dst, in0=y[:, 2:4, :], in1=planes[:, 4:6, :], op=ALU.subtract)
 
@@ -249,32 +257,31 @@ def tile_kanlayer_kernel(tc, x, base_weight_words, base_weight_scales, spline_we
                 in_=t["planes"][:, l0:l1, :].rearrange("p l w -> p (l w)"),
             )
 
+        BASE = L
+        fed = [[] for u in range(UNITS)]
         accd = {}
 
-        def product(u, order=range(L)):
-            bc, bs = units[u]["bc"], units[u]["bs"]
-            acc = accs.tile([P, O], F32, name="acc")
-            nc.tensor.matmul_mx(
-                out=acc[:],
-                lhsT=xc[:, u * P:(u + 1) * P].bitcast(FP8X4),
-                lhsT_scale=xs[:, u * P:(u + 1) * P],
-                rhs=w4[:].bitcast(FP4X4),
-                rhs_scale=w4s[:],
-                start=True,
-                stop=False,
-            )
-            for k, pos in enumerate(order):
-                l = PLANE_AT[pos]
+        def passes(u, which):
+            for k in which:
+                if not fed[u]:
+                    acc = accs.tile([P, O], F32, name="acc")
+                    accd[u] = acc
+                if k == BASE:
+                    lhs, lhs_scale = xc[:, u * P:(u + 1) * P], xs[:, u * P:(u + 1) * P]
+                    rhs, rhs_scale = w4[:].bitcast(FP4X4), w4s[:]
+                else:
+                    lhs, lhs_scale = units[u]["bc"][:, k, :], units[u]["bs"][:, k, :]
+                    rhs, rhs_scale = swc[:, PLANE_AT[k], :].bitcast(FP8X4), sws[:, PLANE_AT[k], :]
                 nc.tensor.matmul_mx(
-                    out=acc[:],
-                    lhsT=bc[:, pos, :].bitcast(FP8X4),
-                    lhsT_scale=bs[:, pos, :],
-                    rhs=swc[:, l, :].bitcast(FP8X4),
-                    rhs_scale=sws[:, l, :],
-                    start=False,
-                    stop=(k == L - 1),
+                    out=accd[u][:],
+                    lhsT=lhs.bitcast(FP8X4),
+                    lhsT_scale=lhs_scale,
+                    rhs=rhs,
+                    rhs_scale=rhs_scale,
+                    start=not fed[u],
+                    stop=(len(fed[u]) == L),
                 )
-            accd[u] = acc
+                fed[u].append(k)
 
         def result(u, parts=1):
             n = O // parts
@@ -286,30 +293,36 @@ def tile_kanlayer_kernel(tc, x, base_weight_words, base_weight_scales, spline_we
         product_at = {5: (0, 1, 2), 6: (3, 4), 7: (5, 6)}
         result_at = {6: (0, 1), 7: (2, 3, 4)}
         H = W // 2
-        x_turn(0, 1, on_vector=True)
         new_unit(0)
         for c0 in (0, H):
-            run(chain_steps(0, c0, c0 + H))
+            xt = tps.tile([P, H], BF16, name="xt", tag="tp")
+            for j in range(2):
+                nc.tensor.transpose(xt[:, j * P:(j + 1) * P], x2[:, c0 // P + j, :], ident_bf[:])
+            run(chain_steps(0, c0, c0 + H, xt[:]))
+            copy_out(xg[:, c0:c0 + H].bitcast(F32), xt[:].bitcast(F32), True)
         x_turn(1, 1, on_vector=True)
-        d_side(0)
+        d_side((0,))
+        x_turn(2, 2, on_vector=True)
         for c0 in (0, H):
             d_big(0, c0, c0 + H)
             run(big_steps(0, c0, c0 + H))
             d_gate(0, c0, c0 + H)
             d_small(0, c0, c0 + H)
         new_unit(1)
+        ready = []
         fills_at = ((0, 1,), (2, 3, 4,), (5, 6, 7,), (8, 9, 10, 11,), (12, 13, 14, 15,), (), (), ())
         run(chain_steps(1), [lambda k=k: w_turn(k) for k in fills_at[0]], 20)
         d_rest(0)
-        x_turn(2)
         d_route(0)
         d_y(0, 0)
         d_y(0, 1)
         for which in (0, 2, 1, 3):
             d_planes(0, which)
         for n in range(1, UNITS):
-            if n in (1, 2):
-                x_turn(2 * n + 2)
+            if n == 1:
+                x_turn(4, 2, on_vector=False)
+            if n == 2:
+                x_turn(6, 2, on_vector=False)
             d_big(n)
             steps = []
             if n + 1 < UNITS:
@@ -330,31 +343,35 @@ def tile_kanlayer_kernel(tc, x, base_weight_words, base_weight_scales, spline_we
                 d_gate(n)
             for k in fills_at[n - 1]:
                 w_quant(k)
+                if k >= L:
+                    ready.append(PLANE_AT.index(k - L))
             if n == 3 + 1:
                 base_quant()
-            for u in {5: (0, 1, 2, 3), 6: (4,), 7: (5,)}.get(n, ()):
-                product(u)
+                ready.append(BASE)
+            for u in ((), (), (), (), (0, 1, 2), (0, 1, 2, 3), (4,), (5,))[n]:
+                passes(u, [k for k in ready if k not in fed[u]])
             if n > 1:
                 for which in (0, 2, 1, 3):
-                    d_planes(n - 1, which)
-            d_side(n)
-            d_rest(n)
+                    d_planes(n - 1, which, on_scalar=(n - 1, which) in ((6, 0),))
+            if n % 2 == 1:
+                d_side(range(n, min(n + 2, UNITS)))
+            d_rest(n, on_scalar=n >= 7)
             d_quant(n - 1)
-            for u in {6: (0, 1), 7: (2, 3)}.get(n, ()):
+            for u in {5: (0,), 6: (1, 2), 7: (3, 4)}.get(n, ()):
                 result(u)
         last = UNITS - 1
         d_route(last)
         d_y(last, 0)
         d_y(last, 1)
-        d_planes(last, 0, on_scalar=False)
+        d_planes(last, 0, on_scalar=True)
         d_planes(last, 1)
         d_planes(last, 2)
         d_quant(last, 0, 4)
         d_planes(last, 3)
         d_quant(last, 4, 6)
         d_quant(last, 6, 8)
-        product(last - 1)
-        product(last)
-        for u in range(4, UNITS - 1):
+        for u in (last - 1, last):
+            passes(u, [k for k in (BASE,) + tuple(range(L)) if k not in fed[u]])
+        for u in range(5, UNITS - 1):
             result(u)
         result(UNITS - 1, 2)

@@ -36,8 +36,8 @@ def tile_kanlayer_kernel(tc, x, base_weight_words, base_weight_scales, spline_we
         loads = ctx.enter_context(tc.tile_pool(name="loads", bufs=4))
         grp = ctx.enter_context(tc.tile_pool(name="grp", bufs=10))
         outs = ctx.enter_context(tc.tile_pool(name="outs", bufs=4))
-        tps = ctx.enter_context(tc.psum_pool(name="tps", bufs=5))
-        accs = ctx.enter_context(tc.psum_pool(name="accs", bufs=3))
+        tps = ctx.enter_context(tc.psum_pool(name="tps", bufs=4))
+        accs = ctx.enter_context(tc.psum_pool(name="accs", bufs=4))
         ctx.enter_context(tc.manual_schedule())
 
         w4s = keep.tile([P, O], U8, name="w4s", align_bytes=64)
@@ -167,9 +167,13 @@ def tile_kanlayer_kernel(tc, x, base_weight_words, base_weight_scales, spline_we
             steps += [step("fold", c, v[:, c, c0:c1], ACT.Abs, 1.0, -1.0) for c in range(2)]
             steps += [step("sq", c, fold[:, c, c0:c1], ACT.Square, S6, -S6) for c in range(2)]
             steps += [step("dist", 0, fold[:, 0, c0:c1], ACT.Abs, 1.0, -1.0)]
-            if u in GATE_ON_SCALAR:
-                steps += [step("gate", c, v[:, c, c0:c1], ACT.Sign, 1.0, -1.0) for c in range(2)]
             return steps
+
+        def gate_steps(u):
+            t = units[u]
+            if u not in GATE_ON_SCALAR:
+                return []
+            return [lambda: nc.scalar.activation(out=t["gate"][:], in_=t["v"][:], func=ACT.Sign, scale=1.0, bias=-1.0)]
 
         def big_steps(u, c0=0, c1=W):
             t = units[u]
@@ -310,7 +314,7 @@ def tile_kanlayer_kernel(tc, x, base_weight_words, base_weight_scales, spline_we
             d_small(0, c0, c0 + H)
         new_unit(1)
         ready = []
-        fills_at = ((0, 1,), (2, 3, 4,), (5, 6, 7,), (8, 9, 10, 11,), (12, 13, 14, 15,), (), (), ())
+        fills_at = ((0, 1,), (2, 3, 4,), (8, 9, 10,), (11, 12, 5,), (13, 6, 14,), (7, 15,), (), ())
         run(chain_steps(1), [lambda k=k: w_turn(k) for k in fills_at[0]], 20)
         d_rest(0)
         d_route(0)
@@ -328,11 +332,13 @@ def tile_kanlayer_kernel(tc, x, base_weight_words, base_weight_scales, spline_we
             if n + 1 < UNITS:
                 new_unit(n + 1)
                 steps = chain_steps(n + 1)
-            steps += big_steps(n)
+            steps += big_steps(n) + gate_steps(n)
             fills = [lambda k=k: w_turn(k) for k in fills_at[n]]
             if n == 3:
                 fills += [lambda k=k: base_turn(k) for k in range(4)]
             run(steps, fills, 20)
+            for u in ((), (), (), (0, 1), (0, 1, 2), (0, 1, 2), (0, 1, 2), ())[n]:
+                passes(u, [k for k in ready if k not in fed[u]])
             if n > 1:
                 d_route(n - 1)
             d_small(n)
@@ -348,16 +354,16 @@ def tile_kanlayer_kernel(tc, x, base_weight_words, base_weight_scales, spline_we
             if n == 3 + 1:
                 base_quant()
                 ready.append(BASE)
-            for u in ((), (), (), (), (0, 1, 2), (0, 1, 2, 3), (4,), (5,))[n]:
-                passes(u, [k for k in ready if k not in fed[u]])
             if n > 1:
                 for which in (0, 2, 1, 3):
                     d_planes(n - 1, which, on_scalar=(n - 1, which) in ((6, 0),))
+            for u in ((), (), (), (), (), (), (0, 1, 2, 3), (4, 5))[n]:
+                passes(u, [k for k in ready if k not in fed[u]])
             if n % 2 == 1:
                 d_side(range(n, min(n + 2, UNITS)))
             d_rest(n, on_scalar=n >= 7)
             d_quant(n - 1)
-            for u in {5: (0,), 6: (1, 2), 7: (3, 4)}.get(n, ()):
+            for u in {6: (0, 1, 2), 7: (3, 4)}.get(n, ()):
                 result(u)
         last = UNITS - 1
         d_route(last)

@@ -21,7 +21,7 @@ FLOPS = 2 * B * O * (I + I * L)
 W = 4 * P
 UNITS = B // P
 S6 = 1.0 / math.sqrt(6.0)
-GATE_ON_SCALAR = (3, 4, 5, 6, 7)
+GATE_ON_SCALAR = (2, 3, 4, 5, 6, 7)
 GAIN = tuple(1.0 if u in GATE_ON_SCALAR else 2.0 for u in range(UNITS))
 FIRST_REUSE = 5
 PLANE_AT = (0, 7, 4, 3, 2, 5, 6, 1)
@@ -34,7 +34,7 @@ def tile_kanlayer_kernel(tc, x, base_weight_words, base_weight_scales, spline_we
         chain = ctx.enter_context(tc.tile_pool(name="chain", bufs=2))
         once = ctx.enter_context(tc.tile_pool(name="once", bufs=1))
         loads = ctx.enter_context(tc.tile_pool(name="loads", bufs=4))
-        grp = ctx.enter_context(tc.tile_pool(name="grp", bufs=10))
+        grp = ctx.enter_context(tc.tile_pool(name="grp", bufs=6))
         outs = ctx.enter_context(tc.tile_pool(name="outs", bufs=4))
         tps = ctx.enter_context(tc.psum_pool(name="tps", bufs=4))
         accs = ctx.enter_context(tc.psum_pool(name="accs", bufs=4))
@@ -105,16 +105,14 @@ def tile_kanlayer_kernel(tc, x, base_weight_words, base_weight_scales, spline_we
             st = tps.tile([P, 8 * P], BF16, name="st", tag="tp")
             for j in range(8):
                 nc.tensor.transpose(st[:, j * P:(j + 1) * P], sw2[2 * half + j // 4][:, j % 4, l:1024:8], ident_bf[:])
-            swg = grp.tile([P, 8 * P], BF16, name="swg", align_bytes=64)
-            nc.scalar.copy(out=swg[:].bitcast(F32), in_=st[:].bitcast(F32))
-            sw_tiles[k] = swg
+            if half == 0:
+                swg = grp.tile([P, 2, 8 * P], BF16, name="swg", align_bytes=64)
+                sw_tiles[l] = swg
+            nc.scalar.copy(out=sw_tiles[l][:, half, :].bitcast(F32), in_=st[:].bitcast(F32))
 
-        def w_quant(k):
-            half, l = divmod(k, L)
+        def w_quant(l):
             nc.vector.quantize_mx(
-                out=swc[:, l, 256 * half:256 * half + 256].bitcast(FP8X4),
-                scales=sws[:, l, 256 * half:256 * half + 256],
-                in_=sw_tiles[k][:],
+                out=swc[:, l, :].bitcast(FP8X4), scales=sws[:, l, :], in_=sw_tiles[l][:].rearrange("p h n -> p (h n)")
             )
 
         def base_turn(n2):
@@ -168,6 +166,15 @@ def tile_kanlayer_kernel(tc, x, base_weight_words, base_weight_scales, spline_we
             steps += [step("sq", c, fold[:, c, c0:c1], ACT.Square, S6, -S6) for c in range(2)]
             steps += [step("dist", 0, fold[:, 0, c0:c1], ACT.Abs, 1.0, -1.0)]
             return steps
+
+        def wide_steps(u):
+            t = units[u]
+            steps = chain_steps(u)
+            return steps[:2] + [
+                lambda: nc.scalar.activation(out=t["fold"][:], in_=t["v"][:], func=ACT.Abs, scale=1.0, bias=-1.0),
+                lambda: nc.scalar.activation(out=t["sq"][:], in_=t["fold"][:], func=ACT.Square, scale=S6, bias=-S6),
+                steps[6],
+            ]
 
         def gate_steps(u):
             t = units[u]
@@ -298,23 +305,27 @@ def tile_kanlayer_kernel(tc, x, base_weight_words, base_weight_scales, spline_we
         result_at = {6: (0, 1), 7: (2, 3, 4)}
         H = W // 2
         new_unit(0)
+        x0 = {}
         for c0 in (0, H):
             xt = tps.tile([P, H], BF16, name="xt", tag="tp")
             for j in range(2):
                 nc.tensor.transpose(xt[:, j * P:(j + 1) * P], x2[:, c0 // P + j, :], ident_bf[:])
             run(chain_steps(0, c0, c0 + H, xt[:]))
-            copy_out(xg[:, c0:c0 + H].bitcast(F32), xt[:].bitcast(F32), True)
+            x0[c0] = xt
         x_turn(1, 1, on_vector=True)
+        for c0 in (0, H):
+            copy_out(xg[:, c0:c0 + H].bitcast(F32), x0[c0][:].bitcast(F32), True)
         d_side((0,))
-        x_turn(2, 2, on_vector=True)
         for c0 in (0, H):
             d_big(0, c0, c0 + H)
             run(big_steps(0, c0, c0 + H))
             d_gate(0, c0, c0 + H)
             d_small(0, c0, c0 + H)
+            if c0 == 0:
+                x_turn(2, 2, on_vector=True)
         new_unit(1)
         ready = []
-        fills_at = ((0, 1,), (2, 3, 4,), (8, 9, 10,), (11, 12, 5,), (13, 6, 14,), (7, 15,), (), ())
+        fills_at = ((), (0, 1,), (2, 3, 4,), (8, 9, 10, 11,), (12, 5, 13, 6,), (14, 7, 15,), (), ())
         run(chain_steps(1), [lambda k=k: w_turn(k) for k in fills_at[0]], 20)
         d_rest(0)
         d_route(0)
@@ -331,8 +342,12 @@ def tile_kanlayer_kernel(tc, x, base_weight_words, base_weight_scales, spline_we
             steps = []
             if n + 1 < UNITS:
                 new_unit(n + 1)
-                steps = chain_steps(n + 1)
-            steps += big_steps(n) + gate_steps(n)
+                steps = wide_steps(n + 1) if n >= 2 else chain_steps(n + 1)
+            big = big_steps(n)
+            if n >= 2:
+                steps = steps[:2] + big[:1] + steps[2:3] + big[1:] + steps[3:] + gate_steps(n)
+            else:
+                steps += big + gate_steps(n)
             fills = [lambda k=k: w_turn(k) for k in fills_at[n]]
             if n == 3:
                 fills += [lambda k=k: base_turn(k) for k in range(4)]
@@ -348,8 +363,8 @@ def tile_kanlayer_kernel(tc, x, base_weight_words, base_weight_scales, spline_we
             if n not in GATE_ON_SCALAR:
                 d_gate(n)
             for k in fills_at[n - 1]:
-                w_quant(k)
                 if k >= L:
+                    w_quant(k - L)
                     ready.append(PLANE_AT.index(k - L))
             if n == 3 + 1:
                 base_quant()
@@ -370,14 +385,15 @@ def tile_kanlayer_kernel(tc, x, base_weight_words, base_weight_scales, spline_we
         d_y(last, 0)
         d_y(last, 1)
         d_planes(last, 0, on_scalar=True)
-        d_planes(last, 1)
+        d_planes(last, 1, on_scalar=True)
         d_planes(last, 2)
-        d_quant(last, 0, 4)
-        d_planes(last, 3)
         d_quant(last, 4, 6)
+        d_planes(last, 3)
+        d_quant(last, 0, 2)
         d_quant(last, 6, 8)
+        d_quant(last, 2, 4)
         for u in (last - 1, last):
-            passes(u, [k for k in (BASE,) + tuple(range(L)) if k not in fed[u]])
+            passes(u, [k for k in (BASE, 4, 5, 0, 1, 6, 7, 2, 3) if k not in fed[u]])
         for u in range(5, UNITS - 1):
             result(u)
         result(UNITS - 1, 2)

@@ -294,16 +294,48 @@ def tile_kanlayer_kernel(tc, x, base_weight_words, base_weight_scales, spline_we
                 )
                 fed[u].append(k)
 
-        def result(u, parts=1):
-            n = O // parts
-            for k in range(parts):
+        def last_product(order):
+            n = O // 4
+            sums = []
+            for j in range(4):
+                part = tps.tile([P, n], F32, name="part", tag="tp")
+                sums.append(part)
+
+            def feed(j, k, start, stop):
+                cols = slice(j * n, (j + 1) * n)
+                if k == BASE:
+                    lhs, lhs_scale = xc[:, last * P:(last + 1) * P], xs[:, last * P:(last + 1) * P]
+                    rhs, rhs_scale = w4[:, 2 * j * n:2 * (j + 1) * n].bitcast(FP4X4), w4s[:, cols]
+                else:
+                    lhs, lhs_scale = units[last]["bc"][:, k, :], units[last]["bs"][:, k, :]
+                    rhs, rhs_scale = swc[:, PLANE_AT[k], cols].bitcast(FP8X4), sws[:, PLANE_AT[k], cols]
+                nc.tensor.matmul_mx(
+                    out=sums[j][:], lhsT=lhs.bitcast(FP8X4), lhsT_scale=lhs_scale, rhs=rhs, rhs_scale=rhs_scale,
+                    start=start, stop=stop,
+                )
+
+            for j in range(4):
+                feed(j, BASE, True, False)
+            for k in order[:-2]:
+                for j in range(4):
+                    feed(j, k, False, False)
+            for j in range(4):
+                feed(j, order[-2], False, False)
+                feed(j, order[-1], False, True)
+            for j in range(4):
                 res = outs.tile([P, n], F32, name="res%d" % n)
-                copy_out(res[:], accd[u][:, k * n:(k + 1) * n], on_vector=(k == 1))
-                nc.sync.dma_start(out=out[u * P:(u + 1) * P, k * n:(k + 1) * n], in_=res[:])
+                copy_out(res[:], sums[j][:], on_vector=(j % 2 == 1))
+                nc.sync.dma_start(out=out[last * P:(last + 1) * P, j * n:(j + 1) * n], in_=res[:])
+
+        def result(u):
+            res = outs.tile([P, O], F32, name="res")
+            nc.scalar.copy(out=res[:], in_=accd[u][:])
+            nc.sync.dma_start(out=out[u * P:(u + 1) * P, :], in_=res[:])
 
         product_at = {5: (0, 1, 2), 6: (3, 4), 7: (5, 6)}
         result_at = {6: (0, 1), 7: (2, 3, 4)}
         H = W // 2
+        last = UNITS - 1
         new_unit(0)
         x0 = {}
         for c0 in (0, H):
@@ -380,7 +412,6 @@ def tile_kanlayer_kernel(tc, x, base_weight_words, base_weight_scales, spline_we
             d_quant(n - 1)
             for u in {6: (0, 1, 2), 7: (3, 4)}.get(n, ()):
                 result(u)
-        last = UNITS - 1
         d_route(last)
         d_y(last, 0)
         d_y(last, 1)
@@ -392,8 +423,7 @@ def tile_kanlayer_kernel(tc, x, base_weight_words, base_weight_scales, spline_we
         d_quant(last, 0, 2)
         d_quant(last, 6, 8)
         d_quant(last, 2, 4)
-        for u in (last - 1, last):
-            passes(u, [k for k in (BASE, 4, 5, 0, 1, 6, 7, 2, 3) if k not in fed[u]])
-        for u in range(5, UNITS - 1):
+        passes(last - 1, [k for k in (BASE,) + tuple(range(L)) if k not in fed[last - 1]])
+        for u in range(5, last):
             result(u)
-        result(UNITS - 1, 2)
+        last_product((4, 5, 0, 1, 6, 7, 2, 3))

@@ -357,7 +357,7 @@ def tile_kanlayer_kernel(tc, x, base_weight_words, base_weight_scales, spline_we
                 x_turn(2, 2, on_vector=True)
         new_unit(1)
         ready = []
-        fills_at = ((), (0, 1,), (2, 3, 4,), (8, 9, 10, 11,), (12, 5, 13, 6,), (14, 7, 15,), (), ())
+        fills_at = ((0,), (1, 2,), (3, 4, 8,), (9, 10, 11, 12,), (5, 13, 6, 14,), (7, 15,), (), ())
         run(chain_steps(1), [lambda k=k: w_turn(k) for k in fills_at[0]], 20)
         d_rest(0)
         d_route(0)
@@ -366,10 +366,6 @@ def tile_kanlayer_kernel(tc, x, base_weight_words, base_weight_scales, spline_we
         for which in (0, 2, 1, 3):
             d_planes(0, which)
         for n in range(1, UNITS):
-            if n == 1:
-                x_turn(4, 2, on_vector=False)
-            if n == 2:
-                x_turn(6, 2, on_vector=False)
             d_big(n)
             steps = []
             if n + 1 < UNITS:
@@ -381,6 +377,8 @@ def tile_kanlayer_kernel(tc, x, base_weight_words, base_weight_scales, spline_we
             else:
                 steps += big + gate_steps(n)
             fills = [lambda k=k: w_turn(k) for k in fills_at[n]]
+            if n in (1, 2):
+                fills = [lambda: x_turn(4 if n == 1 else 6)] + fills
             if n == 3:
                 fills += [lambda k=k: base_turn(k) for k in range(4)]
             run(steps, fills, 20)

@@ -359,8 +359,8 @@ def tile_kanlayer_kernel(tc, x, base_weight_words, base_weight_scales, spline_we
         ready = []
         fills_at = ((0,), (1, 2,), (3, 4, 8,), (9, 10, 11, 12,), (5, 13, 6, 14,), (7, 15,), (), ())
         run(chain_steps(1), [lambda k=k: w_turn(k) for k in fills_at[0]], 20)
-        d_rest(0)
         d_route(0)
+        d_rest(0)
         d_y(0, 0)
         d_y(0, 1)
         for which in (0, 2, 1, 3):
@@ -404,24 +404,26 @@ def tile_kanlayer_kernel(tc, x, base_weight_words, base_weight_scales, spline_we
                     d_planes(n - 1, which, on_scalar=(n - 1, which) in ((6, 0),))
             for u in ((), (), (), (), (), (), (0, 1, 2, 3), (4, 5))[n]:
                 passes(u, [k for k in ready if k not in fed[u]])
-            if n % 2 == 1:
+            if n % 2 == 1 and n < last:
                 d_side(range(n, min(n + 2, UNITS)))
-            d_rest(n, on_scalar=n >= 7)
+            d_rest(n, on_scalar=n == last)
+            if n == last:
+                d_route(last)
             d_quant(n - 1)
             for u in {6: (0, 1, 2), 7: (3, 4)}.get(n, ()):
                 result(u)
-        d_route(last)
         d_y(last, 0)
         d_y(last, 1)
         d_planes(last, 0, on_scalar=True)
         d_planes(last, 1, on_scalar=True)
+        d_side((last,))
         d_planes(last, 2)
+        d_quant(last, 0, 2)
         d_quant(last, 4, 6)
         d_planes(last, 3)
-        d_quant(last, 0, 2)
-        d_quant(last, 6, 8)
         d_quant(last, 2, 4)
+        d_quant(last, 6, 8)
         passes(last - 1, [k for k in (BASE,) + tuple(range(L)) if k not in fed[last - 1]])
         for u in range(5, last):
             result(u)
-        last_product((4, 5, 0, 1, 6, 7, 2, 3))
+        last_product((0, 1, 4, 5, 2, 3, 6, 7))

@@ -382,14 +382,14 @@ def tile_kanlayer_kernel(tc, x, base_weight_words, base_weight_scales, spline_we
             if n == 3:
                 fills += [lambda k=k: base_turn(k) for k in range(4)]
             run(steps, fills, 20)
-            for u in ((), (), (), (0, 1), (0, 1, 2), (0, 1, 2), (0, 1, 2), ())[n]:
+            for u in ((), (), (), (0, 1), (0, 1, 2), (0, 1, 2, 3), (0, 1, 2, 3), ())[n]:
                 passes(u, [k for k in ready if k not in fed[u]])
             if n > 1:
                 d_route(n - 1)
             d_small(n)
             if n > 1:
-                d_y(n - 1, 0)
                 d_y(n - 1, 1)
+                d_y(n - 1, 0)
             if n not in GATE_ON_SCALAR:
                 d_gate(n)
             for k in fills_at[n - 1]:
@@ -400,7 +400,7 @@ def tile_kanlayer_kernel(tc, x, base_weight_words, base_weight_scales, spline_we
                 base_quant()
                 ready.append(BASE)
             if n > 1:
-                for which in (0, 2, 1, 3):
+                for which in (2, 0, 1, 3):
                     d_planes(n - 1, which, on_scalar=(n - 1, which) in ((6, 0),))
             for u in ((), (), (), (), (), (), (0, 1, 2, 3), (4, 5))[n]:
                 passes(u, [k for k in ready if k not in fed[u]])

from contextlib import ExitStack
import math

import concourse.mybir as mybir
from concourse.masks import make_identity

F32 = mybir.dt.float32
BF16 = mybir.dt.bfloat16
U8 = mybir.dt.uint8
U32 = mybir.dt.uint32
I32 = mybir.dt.int32
FP8X4 = mybir.dt.float8_e4m3fn_x4
FP4X4 = mybir.dt.float4_e2m1fn_x4
ALU = mybir.AluOpType
ACT = mybir.ActivationFunctionType

P = 128
B, I, O, L = 1024, 512, 512, 8
FLOPS = 2 * B * O * (I + I * L)

W = 4 * P
UNITS = B // P
S6 = 1.0 / math.sqrt(6.0)
GATE_ON_SCALAR = (2, 3, 4, 5, 6, 7)
GAIN = tuple(1.0 if u in GATE_ON_SCALAR else 2.0 for u in range(UNITS))
FIRST_REUSE = 5
PLANE_AT = (0, 7, 4, 3, 2, 5, 6, 1)


def tile_kanlayer_kernel(tc, x, base_weight_words, base_weight_scales, spline_weight, out):
    nc = tc.nc
    with ExitStack() as ctx:
        keep = ctx.enter_context(tc.tile_pool(name="keep", bufs=1))
        chain = ctx.enter_context(tc.tile_pool(name="chain", bufs=2))
        once = ctx.enter_context(tc.tile_pool(name="once", bufs=1))
        loads = ctx.enter_context(tc.tile_pool(name="loads", bufs=4))
        grp = ctx.enter_context(tc.tile_pool(name="grp", bufs=6))
        outs = ctx.enter_context(tc.tile_pool(name="outs", bufs=4))
        tps = ctx.enter_context(tc.psum_pool(name="tps", bufs=4))
        accs = ctx.enter_context(tc.psum_pool(name="accs", bufs=4))
        ctx.enter_context(tc.manual_schedule())

        w4s = keep.tile([P, O], U8, name="w4s", align_bytes=64)
        nc.vector.memset(w4s[:].bitcast(I32), 0)
        ident_bf = keep.tile([P, P], BF16, name="ident_bf")
        make_identity(nc, ident_bf[:])
        ident_f = keep.tile([P, P], F32, name="ident_f")
        make_identity(nc, ident_f[:])

        x2 = keep.tile([P, 32, P], BF16, name="x2")
        x2_src = x.rearrange("(n bl) (t p) -> (bl t) n p", bl=32, t=4)
        sw2 = []
        sw2_src = spline_weight.rearrange("(m ol) (t p) l -> (ol t) m (p l)", ol=32, t=4)
        xb = keep.tile([P, 8, I], BF16, name="xb")
        w4 = keep.tile([P, 2 * O], U8, name="w4", align_bytes=64)

        def load_x2(a, b):
            nc.sync.dma_start(out=x2[:, a:b, :], in_=x2_src[:, a:b, :])

        def load_sw(g):
            quarter = loads.tile([P, 4, 1024], BF16, name="quarter", align_bytes=64)
            nc.sync.dma_start(out=quarter[:], in_=sw2_src[:, 4 * g:4 * g + 4, :])
            sw2.append(quarter)

        load_x2(0, 2)
        load_x2(2, 4)
        load_x2(4, 8)
        load_x2(8, 16)
        load_sw(0)
        load_sw(1)
        load_x2(16, 32)
        load_sw(2)
        load_sw(3)
        nc.sync.dma_start(out=xb[:], in_=x.rearrange("(n b) i -> b n i", b=P))
        nc.sync.dma_start(out=w4[:].bitcast(I32), in_=base_weight_words[0].bitcast(I32))
        for q in range(4):
            nc.sync.dma_start(
                out=w4s[32 * q:32 * q + 4, :].bitcast(I32),
                in_=base_weight_scales[0, 4 * q:4 * q + 4, :].bitcast(I32),
            )

        xg = keep.tile([P, 4 * B], BF16, name="xg", align_bytes=64)
        swc = keep.tile([P, L, O], U32, name="swc", align_bytes=64)
        sws = keep.tile([P, L, O], U8, name="sws", align_bytes=64)
        xc = keep.tile([P, B], U32, name="xc", align_bytes=64)
        xs = keep.tile([P, B], U8, name="xs", align_bytes=64)
        xbg = keep.tile([P, B, 2], F32, name="xbg", align_bytes=64)

        def copy_out(out, in_, on_vector):
            if on_vector:
                nc.vector.tensor_copy(out=out, in_=in_)
            else:
                nc.scalar.copy(out=out, in_=in_)

        def x_turn(u0, units=2, on_vector=False):
            xt = tps.tile([P, units * W], BF16, name="xt", tag="tp")
            for j in range(4 * units):
                nc.tensor.transpose(xt[:, j * P:(j + 1) * P], x2[:, 4 * u0 + j, :], ident_bf[:])
            copy_out(xg[:, u0 * W:(u0 + units) * W].bitcast(F32), xt[:].bitcast(F32), on_vector)

        sw_tiles = {}

        def w_turn(k):
            half, l = divmod(k, L)
            st = tps.tile([P, 8 * P], BF16, name="st", tag="tp")
            for j in range(8):
                nc.tensor.transpose(st[:, j * P:(j + 1) * P], sw2[2 * half + j // 4][:, j % 4, l:1024:8], ident_bf[:])
            if half == 0:
                swg = grp.tile([P, 2, 8 * P], BF16, name="swg", align_bytes=64)
                sw_tiles[l] = swg
            nc.scalar.copy(out=sw_tiles[l][:, half, :].bitcast(F32), in_=st[:].bitcast(F32))

        def w_quant(l):
            nc.vector.quantize_mx(
                out=swc[:, l, :].bitcast(FP8X4), scales=sws[:, l, :], in_=sw_tiles[l][:].rearrange("p h n -> p (h n)")
            )

        def base_turn(n2):
            bt = tps.tile([P, 2, 2, P], F32, name="bt", tag="tp")
            for dn in range(2):
                words = xb[:, 2 * n2 + dn, :].bitcast(F32)
                for u in range(2):
                    nc.tensor.transpose(bt[:, dn, u, :], words[:, u:256:2], ident_f[:])
            nc.scalar.copy(
                out=xbg[:, 2 * n2 * P:(2 * n2 + 2) * P, :].rearrange("p (dn b) u -> p dn b u", dn=2),
                in_=bt[:].rearrange("p dn u b -> p dn b u"),
            )

        def base_quant():
            nc.vector.quantize_mx(
                out=xc[:].bitcast(FP8X4),
                scales=xs[:],
                in_=xbg[:].rearrange("p b u -> p (b u)").bitcast(BF16),
            )

        units = {}
        sides = {}

        def new_unit(u):
            t = {}
            for name, pool, rows, dtype in (
                ("v", chain, 2, F32), ("fold", chain, 2, F32), ("dist", chain, 1, F32), ("sq", chain, 2, F32),
                ("big32", chain, 2, F32), ("big", chain, 2, BF16), ("gate", chain, 2, BF16), ("small", chain, 2, BF16),
                ("rest", once, 2, BF16), ("y", once, 4, BF16), ("planes", once, L, BF16),
            ):
                t[name] = pool.tile([P, rows, W], dtype, name=name, align_bytes=64)
            if u < FIRST_REUSE:
                bc = keep.tile([P, L, P], U32, name="bc%d" % u, align_bytes=64)
            else:
                bc = loads.tile([P, L, P], U32, name="bc", tag="quarter", align_bytes=64)
            bs = keep.tile([P, L, P], U8, name="bs%d" % u, align_bytes=64)
            t["bc"], t["bs"] = bc, bs
            units[u] = t

        def chain_steps(u, c0=0, c1=W, x_from=None):
            xk = xg[:, u * W + c0:u * W + c1] if x_from is None else x_from
            t = units[u]

            def step(name, row, in_, func, scale, bias):
                out_ = t[name][:, row, c0:c1]
                return lambda: nc.scalar.activation(out=out_, in_=in_, func=func, scale=scale, bias=bias)

            v, fold = t["v"], t["fold"]
            steps = [step("v", c, xk, ACT.Abs, 2.5, c - 0.5) for c in range(2)]
            steps += [step("fold", c, v[:, c, c0:c1], ACT.Abs, 1.0, -1.0) for c in range(2)]
            steps += [step("sq", c, fold[:, c, c0:c1], ACT.Square, S6, -S6) for c in range(2)]
            steps += [step("dist", 0, fold[:, 0, c0:c1], ACT.Abs, 1.0, -1.0)]
            return steps

        def wide_steps(u):
            t = units[u]
            steps = chain_steps(u)
            return steps[:2] + [
                lambda: nc.scalar.activation(out=t["fold"][:], in_=t["v"][:], func=ACT.Abs, scale=1.0, bias=-1.0),
                lambda: nc.scalar.activation(out=t["sq"][:], in_=t["fold"][:], func=ACT.Square, scale=S6, bias=-S6),
                steps[6],
            ]

        def gate_steps(u):
            t = units[u]
            if u not in GATE_ON_SCALAR:
                return []
            return [lambda: nc.scalar.activation(out=t["gate"][:], in_=t["v"][:], func=ACT.Sign, scale=1.0, bias=-1.0)]

        def big_steps(u, c0=0, c1=W):
            t = units[u]

            def step(c):
                return lambda: nc.scalar.activation(out=t["big"][:, c, c0:c1], in_=t["big32"][:, c, c0:c1], func=ACT.Copy,
                                                    scale=(3.0 if c == 0 else -3.0) * GAIN[u], bias=2.0 / 3.0 * GAIN[u])

            return [step(0), step(1)]

        def run(steps, fills=(), every=2):
            fills = list(fills)
            for k, step in enumerate(steps):
                step()
                if k % every == every - 1 and fills:
                    fills[0]()
                    fills = fills[1:]
            for fill in fills:
                fill()

        def d_big(u, c0=0, c1=W):
            t = units[u]
            for c in range(2):
                nc.vector.scalar_tensor_tensor(out=t["big32"][:, c, c0:c1], in0=t["dist"][:, 0, c0:c1],
                                               scalar=(-2.0 if c == 0 else 1.0), in1=t["sq"][:, c, c0:c1],
                                               op0=ALU.add, op1=ALU.mult)

        def d_small(u, c0=0, c1=W):
            t = units[u]
            nc.vector.scalar_tensor_tensor(out=t["small"][:, :, c0:c1], in0=t["fold"][:, :, c0:c1], scalar=1.0,
                                           in1=t["sq"][:, :, c0:c1], op0=ALU.subtract, op1=ALU.mult)

        def d_gate(u, c0=0, c1=W):
            t = units[u]
            nc.vector.tensor_scalar(out=t["gate"][:, :, c0:c1], in0=t["v"][:, :, c0:c1], scalar1=1.0, scalar2=0.5,
                                    op0=ALU.is_ge, op1=ALU.subtract)

        def d_side(us):
            k = len(us)
            xk = xg[:, us[0] * W:(us[0] + k) * W].rearrange("p (k w) -> p k w", w=W)
            side = once.tile([P, k, 2, W], BF16, name="side")
            nc.vector.tensor_scalar(out=side[:, :, 0, :], in0=xk, scalar1=0.2, scalar2=1.0, op0=ALU.is_lt, op1=ALU.mult)
            nc.vector.tensor_scalar(out=side[:, :, 1, :], in0=xk, scalar1=-0.2, scalar2=1.0, op0=ALU.is_ge, op1=ALU.mult)
            for j, u in enumerate(us):
                sides[u] = side[:, j]

        def d_rest(u, on_scalar=False):
            t = units[u]
            if on_scalar:
                nc.scalar.activation(out=t["rest"][:], in_=t["small"][:], func=ACT.Relu, scale=-1.0)
            else:
                nc.vector.tensor_scalar(out=t["rest"][:], in0=t["small"][:], scalar1=-1.0, scalar2=0.0, op0=ALU.mult, op1=ALU.max)

        def d_route(u):
            t = units[u]
            nc.vector.tensor_tensor(out=t["big"][:], in0=t["big"][:], in1=t["gate"][:], op=ALU.mult)

        def d_y(u, slot):
            t = units[u]
            if slot == 0:
                nc.vector.tensor_tensor(out=t["y"][:, 0:2, :], in0=t["small"][:], in1=t["big"][:], op=ALU.min)
            else:
                nc.vector.tensor_tensor(out=t["y"][:, 2:4, :], in0=t["rest"][:], in1=t["big"][:], op=ALU.max)

        def d_planes(u, which, on_scalar=False):
            t = units[u]
            y, planes = t["y"], t["planes"]
            dst = planes[:, 2 * which:2 * which + 2, :]
            if which < 2:
                sign = 1.0 - 2.0 * which
                if on_scalar:
                    nc.scalar.activation(out=dst, in_=y[:, 0:2, :], func=ACT.Relu, scale=sign)
                else:
                    nc.vector.tensor_scalar(out=dst, in0=y[:, 0:2, :], scalar1=sign, scalar2=0.0, op0=ALU.mult, op1=ALU.max)
            elif which == 2:
                nc.vector.tensor_tensor(out=dst, in0=y[:, 2:4, :], in1=sides[u], op=ALU.mult)
            else:
                nc.vector.tensor_tensor(out=dst, in0=y[:, 2:4, :], in1=planes[:, 4:6, :], op=ALU.subtract)

        def d_quant(u, l0=0, l1=L):
            t = units[u]
            nc.vector.quantize_mx(
                out=t["bc"][:, l0:l1, :].rearrange("p l w -> p (l w)").bitcast(FP8X4),
                scales=t["bs"][:, l0:l1, :].rearrange("p l w -> p (l w)"),
                in_=t["planes"][:, l0:l1, :].rearrange("p l w -> p (l w)"),
            )

        BASE = L
        fed = [[] for u in range(UNITS)]
        accd = {}

        def passes(u, which):
            for k in which:
                if not fed[u]:
                    acc = accs.tile([P, O], F32, name="acc")
                    accd[u] = acc
                if k == BASE:
                    lhs, lhs_scale = xc[:, u * P:(u + 1) * P], xs[:, u * P:(u + 1) * P]
                    rhs, rhs_scale = w4[:].bitcast(FP4X4), w4s[:]
                else:
                    lhs, lhs_scale = units[u]["bc"][:, k, :], units[u]["bs"][:, k, :]
                    rhs, rhs_scale = swc[:, PLANE_AT[k], :].bitcast(FP8X4), sws[:, PLANE_AT[k], :]
                nc.tensor.matmul_mx(
                    out=accd[u][:],
                    lhsT=lhs.bitcast(FP8X4),
                    lhsT_scale=lhs_scale,
                    rhs=rhs,
                    rhs_scale=rhs_scale,
                    start=not fed[u],
                    stop=(len(fed[u]) == L),
                )
                fed[u].append(k)

        def last_product(order):
            n = O // 4
            sums = []
            for j in range(4):
                part = tps.tile([P, n], F32, name="part", tag="tp")
                sums.append(part)

            def feed(j, k, start, stop):
                cols = slice(j * n, (j + 1) * n)
                if k == BASE:
                    lhs, lhs_scale = xc[:, last * P:(last + 1) * P], xs[:, last * P:(last + 1) * P]
                    rhs, rhs_scale = w4[:, 2 * j * n:2 * (j + 1) * n].bitcast(FP4X4), w4s[:, cols]
                else:
                    lhs, lhs_scale = units[last]["bc"][:, k, :], units[last]["bs"][:, k, :]
                    rhs, rhs_scale = swc[:, PLANE_AT[k], cols].bitcast(FP8X4), sws[:, PLANE_AT[k], cols]
                nc.tensor.matmul_mx(
                    out=sums[j][:], lhsT=lhs.bitcast(FP8X4), lhsT_scale=lhs_scale, rhs=rhs, rhs_scale=rhs_scale,
                    start=start, stop=stop,
                )

            for j in range(4):
                feed(j, BASE, True, False)
            for k in order[:-2]:
                for j in range(4):
                    feed(j, k, False, False)
            for j in range(4):
                feed(j, order[-2], False, False)
                feed(j, order[-1], False, True)
            for j in range(4):
                res = outs.tile([P, n], F32, name="res%d" % n)
                copy_out(res[:], sums[j][:], on_vector=(j % 2 == 1))
                nc.sync.dma_start(out=out[last * P:(last + 1) * P, j * n:(j + 1) * n], in_=res[:])

        def result(u):
            res = outs.tile([P, O], F32, name="res")
            nc.scalar.copy(out=res[:], in_=accd[u][:])
            nc.sync.dma_start(out=out[u * P:(u + 1) * P, :], in_=res[:])

        product_at = {5: (0, 1, 2), 6: (3, 4), 7: (5, 6)}
        result_at = {6: (0, 1), 7: (2, 3, 4)}
        H = W // 2
        last = UNITS - 1
        new_unit(0)
        x0 = {}
        for c0 in (0, H):
            xt = tps.tile([P, H], BF16, name="xt", tag="tp")
            for j in range(2):
                nc.tensor.transpose(xt[:, j * P:(j + 1) * P], x2[:, c0 // P + j, :], ident_bf[:])
            run(chain_steps(0, c0, c0 + H, xt[:]))
            x0[c0] = xt
        x_turn(1, 1, on_vector=True)
        for c0 in (0, H):
            copy_out(xg[:, c0:c0 + H].bitcast(F32), x0[c0][:].bitcast(F32), True)
        d_side((0,))
        for c0 in (0, H):
            d_big(0, c0, c0 + H)
            run(big_steps(0, c0, c0 + H))
            d_gate(0, c0, c0 + H)
            d_small(0, c0, c0 + H)
            if c0 == 0:
                x_turn(2, 2, on_vector=True)
        new_unit(1)
        ready = []
        fills_at = ((0,), (1, 2,), (3, 4, 8,), (9, 10, 11, 12,), (5, 13, 6, 14,), (7, 15,), (), ())
        run(chain_steps(1), [lambda k=k: w_turn(k) for k in fills_at[0]], 20)
        d_route(0)
        d_rest(0)
        d_y(0, 0)
        d_y(0, 1)
        for which in (0, 2, 1, 3):
            d_planes(0, which)
        for n in range(1, UNITS):
            d_big(n)
            steps = []
            if n + 1 < UNITS:
                new_unit(n + 1)
                steps = wide_steps(n + 1) if n >= 2 else chain_steps(n + 1)
            big = big_steps(n)
            if n >= 2:
                steps = steps[:2] + big[:1] + steps[2:3] + big[1:] + steps[3:] + gate_steps(n)
            else:
                steps += big + gate_steps(n)
            fills = [lambda k=k: w_turn(k) for k in fills_at[n]]
            if n in (1, 2):
                fills = [lambda: x_turn(4 if n == 1 else 6)] + fills
            if n == 3:
                fills += [lambda k=k: base_turn(k) for k in range(4)]
            run(steps, fills, 20)
            for u in ((), (), (), (0, 1), (0, 1, 2), (0, 1, 2, 3), (0, 1, 2, 3), ())[n]:
                passes(u, [k for k in ready if k not in fed[u]])
            if n > 1:
                d_route(n - 1)
            d_small(n)
            if n > 1:
                d_y(n - 1, 1)
                d_y(n - 1, 0)
            if n not in GATE_ON_SCALAR:
                d_gate(n)
            for k in fills_at[n - 1]:
                if k >= L:
                    w_quant(k - L)
                    ready.append(PLANE_AT.index(k - L))
            if n == 3 + 1:
                base_quant()
                ready.append(BASE)
            if n > 1:
                for which in (2, 0, 1, 3):
                    d_planes(n - 1, which, on_scalar=(n - 1, which) in ((6, 0),))
            for u in ((), (), (), (), (), (), (0, 1, 2, 3), (4, 5))[n]:
                passes(u, [k for k in ready if k not in fed[u]])
            if n % 2 == 1 and n < last:
                d_side(range(n, min(n + 2, UNITS)))
            d_rest(n, on_scalar=n == last)
            if n == last:
                d_route(last)
            d_quant(n - 1)
            for u in {6: (0, 1, 2), 7: (3, 4)}.get(n, ()):
                result(u)
        d_y(last, 0)
        d_y(last, 1)
        d_planes(last, 0, on_scalar=True)
        d_planes(last, 1, on_scalar=True)
        d_side((last,))
        d_planes(last, 2)
        d_quant(last, 0, 2)
        d_quant(last, 4, 6)
        d_planes(last, 3)
        d_quant(last, 2, 4)
        d_quant(last, 6, 8)
        passes(last - 1, [k for k in (BASE,) + tuple(range(L)) if k not in fed[last - 1]])
        for u in range(5, last):
            result(u)
        last_product((0, 1, 4, 5, 2, 3, 6, 7))
